import numpy as np
import ml_dtypes


def mxq(x, axis, fmt="e4m3"):
    dtype, down = {"e4m3": (ml_dtypes.float8_e4m3fn, 7), "e5m2": (ml_dtypes.float8_e5m2, 14)}[fmt]
    v = np.moveaxis(np.asarray(x, np.float32).astype(ml_dtypes.bfloat16).astype(np.float64), axis, -1)
    blocks = v.reshape(v.shape[:-1] + (-1, 32))
    amax = np.abs(blocks).max(-1, keepdims=True)
    byte = np.maximum(np.where(amax > 0, np.frexp(amax)[1] - 1 + 127, 0) - down, 1)
    scale = np.exp2(byte - 127.0)
    codes = (blocks / scale).astype(np.float32).astype(dtype).astype(np.float64)
    return np.moveaxis((codes * scale).reshape(v.shape), -1, axis)


WIDE = False


def mx_kscale(k):
    if not WIDE:
        return np.ones(k)
    levels = np.array([10, -10, 5, -5, 0])
    if k % 512:
        return np.exp2(np.random.permutation(np.resize(levels, k // 32))).repeat(32)
    a = np.empty((k // 512, 16))
    for p in range(k // 512):
        a[p, :8] = np.random.permutation(np.resize(levels, 8))
        for g in range(8):
            far = levels[np.abs(levels - a[p, g]) >= 10]
            a[p, g + 8] = far[np.random.randint(len(far))]
    return np.exp2(a.ravel()).repeat(32)


BF16 = ml_dtypes.bfloat16


def bf(x):
    return np.asarray(x, np.float32).astype(BF16)


def f64(x):
    return np.asarray(x).astype(np.float64)


B, S, D, QR, KR, H, NOPE, ROPE, VD = 2, 2048, 1024, 1536, 512, 2, 128, 64, 128
EPS = 1e-6
THETA = 10000.0
LAT = 3.0 * np.sqrt(EPS)


def rmsnorm(x, w):
    var = np.mean(x * x, axis=-1, keepdims=True)
    return w * (x * (1.0 / np.sqrt(var + EPS)))


def rope_cos_sin(seq_len):
    inv_freq = 1.0 / (THETA ** (f64(np.arange(0, ROPE, 2)) / ROPE))
    t = f64(np.arange(seq_len))
    freqs = np.outer(t, inv_freq)
    emb = np.concatenate([freqs, freqs], -1)
    return np.cos(emb), np.sin(emb)


def rotate_half(x):
    x1, x2 = x[..., : x.shape[-1] // 2], x[..., x.shape[-1] // 2 :]
    return np.concatenate([-x2, x1], axis=-1)


def setup_inputs():
    s, t = mx_kscale(D), mx_kscale(KR)
    return {"hidden_states": bf(np.random.standard_normal((B, S, D)) * s),
            "kv_a_w_ckv": bf(np.random.standard_normal((KR, D)) * LAT / np.sqrt(D) / s[None, :]),
            "k_pe_raw": bf(np.random.standard_normal((B, S, ROPE))),
            "kv_a_ln_w": bf((1.0 + 0.1 * np.random.standard_normal(KR)) * t),
            "kv_b_w": bf(np.random.standard_normal((H * (NOPE + VD), KR)) / np.sqrt(KR) / t[None, :])}


def reference(hidden_states, kv_a_w_ckv, k_pe_raw, kv_a_ln_w, kv_b_w):
    ckv = mxq(f64(hidden_states), 2, "e4m3") @ mxq(f64(kv_a_w_ckv), 1, "e4m3").T
    ckv_n = rmsnorm(ckv, f64(kv_a_ln_w))
    kv = mxq(ckv_n, 2, "e4m3") @ mxq(f64(kv_b_w), 1, "e4m3").T
    kv = kv.reshape(B, S, H, NOPE + VD).transpose(0, 2, 1, 3)
    k_nope, v = kv[..., :NOPE], kv[..., NOPE:]
    k_pe = f64(k_pe_raw).reshape(B, 1, S, ROPE)
    cos, sin = rope_cos_sin(S)
    cos, sin = cos[None, None], sin[None, None]
    k_pe = k_pe * cos + rotate_half(k_pe) * sin
    key_s = np.concatenate([k_nope, np.broadcast_to(k_pe, (B, H, S, ROPE))], -1)
    return key_s, v

@@ -1,0 +1,293 @@
+from contextlib import ExitStack
+import math
+
+import concourse.mybir as mybir
+from concourse.masks import make_identity
+
+FLOPS = 2 * 4096 * 1024 * 512 + 2 * 4096 * 512 * 512
+
+F32 = mybir.dt.float32
+BF16 = mybir.dt.bfloat16
+I32 = mybir.dt.int32
+U32 = mybir.dt.uint32
+U8 = mybir.dt.uint8
+FP8X4 = mybir.dt.float8_e4m3fn_x4
+ALU = mybir.AluOpType
+ACT = mybir.ActivationFunctionType
+
+P = 128
+EPS = 1e-6
+THETA = 10000.0
+N_TILES = 32
+
+
+def tile_modelnew_pb_t_kernel(tc, hidden_states, kv_a_w_ckv, k_pe_raw, kv_a_ln_w, kv_b_w, out_0, out_1):
+    nc = tc.nc
+    with ExitStack() as ctx:
+        const = ctx.enter_context(tc.tile_pool(name="const", bufs=1))
+        work = ctx.enter_context(tc.tile_pool(name="work", bufs=6))
+        outp = ctx.enter_context(tc.tile_pool(name="outp", bufs=4))
+        tpp = ctx.enter_context(tc.psum_pool(name="tpp", bufs=3))
+        mxp = ctx.enter_context(tc.psum_pool(name="mxp", bufs=5))
+        ctx.enter_context(tc.manual_schedule())
+
+        s_i = const.tile([P, 16], I32, name="s_i")
+        nc.gpsimd.iota(s_i[:], pattern=[[512, 4], [1, 4]], base=0, channel_multiplier=4)
+        ident_f = const.tile([P, P], F32, name="ident_f")
+        make_identity(nc, ident_f[:])
+
+        one = const.tile([P, 1], F32, name="one")
+        nc.vector.memset(one[:], 1.0)
+        warm0 = const.tile([P, 1], F32, name="warm0")
+        nc.scalar.activation(out=warm0[:], in_=one[:], func=ACT.Sin)
+
+        hs_v = hidden_states.flatten_outer_dims().rearrange("(c p j) d -> c p (j d)", p=P, j=4)
+        wa_sb = []
+        for a in range(4):
+            wa_a = const.tile([P, 1024], BF16, name="wa%d" % a)
+            wa_sb.append(wa_a)
+        wb_sb = const.tile([P, 4, 512], BF16, name="wb_sb")
+        kpe = const.tile([P, 8, 256], BF16, name="kpe")
+        hs_sb = []
+        for h2 in range(16):
+            hs_c = const.tile([P, 2, 1024], BF16, name="hs%d" % h2)
+            hs_sb.append(hs_c)
+
+        def load_hs(c):
+            for e in range(2):
+                nc.sync.dma_start(out=hs_sb[2 * c + e][:].rearrange("p j d -> p (j d)"), in_=hs_v[c][:, e * 2048:(e + 1) * 2048])
+
+        def load_first_tiles():
+            for j in range(2):
+                nc.sync.dma_start(out=hs_sb[0][:, j, :], in_=hs_v[0][:, j * 1024:(j + 1) * 1024])
+            nc.sync.dma_start(out=hs_sb[1][:].rearrange("p j d -> p (j d)"), in_=hs_v[0][:, 2048:4096])
+
+        wa_v = kv_a_w_ckv.rearrange("(p a) d -> a p d", a=4)
+        for a in range(4):
+            nc.sync.dma_start(out=wa_sb[a][:], in_=wa_v[a])
+        load_first_tiles()
+        w_pt = const.tile([P, 4], BF16, name="w_pt")
+        nc.sync.dma_start(out=w_pt[:], in_=kv_a_ln_w.rearrange("(p t) -> p t", t=4))
+        nc.sync.dma_start(out=wb_sb[:], in_=kv_b_w.rearrange("(a p) k -> p a k", p=P))
+        load_hs(1)
+        nc.sync.dma_start(out=kpe[:], in_=k_pe_raw.flatten_outer_dims().rearrange("(c p j) r -> p c (j r)", p=P, j=4))
+        for c in range(2, 8):
+            load_hs(c)
+
+        s_f = const.tile([P, 16], F32, name="s_f")
+        nc.vector.tensor_copy(out=s_f[:], in_=s_i[:])
+        fr = const.tile([P, 32], F32, name="fr")
+        nc.vector.memset(fr[:, 0:1], 1.0)
+        for m in range(5):
+            n = 1 << m
+            nc.vector.tensor_scalar(out=fr[:, n:2 * n], in0=fr[:, 0:n], scalar1=THETA ** (-n / 32.0), scalar2=None, op0=ALU.mult)
+        nc.vector.tensor_scalar(out=fr[:], in0=fr[:], scalar1=1.0 / (2.0 * math.pi), scalar2=None, op0=ALU.mult)
+        ang = const.tile([P, 2, 16, 32], F32, name="ang")
+        nc.vector.tensor_tensor(out=ang[:, 0], in0=s_f[:].unsqueeze(2).to_broadcast([P, 16, 32]),
+                                in1=fr[:].unsqueeze(1).to_broadcast([P, 16, 32]), op=ALU.mult)
+        nc.vector.tensor_scalar(out=ang[:, 1], in0=ang[:, 0], scalar1=0.25, scalar2=None, op0=ALU.add)
+        ang_f = ang[:].rearrange("p a s i -> p (a s i)")
+        q_i = const.tile([P, 1024], I32, name="q_i")
+        nc.vector.tensor_copy(out=q_i[:], in_=ang_f)
+        k_f = const.tile([P, 1024], F32, name="k_f")
+        nc.vector.tensor_copy(out=k_f[:], in_=q_i[:])
+        nc.vector.tensor_tensor(out=ang_f, in0=ang_f, in1=k_f[:], op=ALU.subtract)
+        eps_t = const.tile([P, 1], F32, name="eps_t")
+        nc.vector.memset(eps_t[:], 1.0)
+        nc.vector.tensor_scalar(out=eps_t[:], in0=eps_t[:], scalar1=EPS, scalar2=None, op0=ALU.mult)
+        tab = const.tile([P, 2, 16, 32], F32, name="tab")
+        nsin = const.tile([P, 16, 32], F32, name="nsin")
+
+        def word_transposes(xt, words):
+            for g in range(2):
+                for u in range(2):
+                    nc.tensor.transpose(xt[:, g, u, :], words[:, 256 * g + u:256 * (g + 1):2], ident_f[:])
+
+        wa_grp = const.tile([P, 2, 512, 2], F32, name="wa_grp", align_bytes=64)
+        wa_c = const.tile([P, 2, 512], U32, name="wa_c", align_bytes=64)
+        wa_s = const.tile([P, 2, 512], U8, name="wa_s", align_bytes=64)
+        for a in range(4):
+            xt = tpp.tile([P, 2, 2, P], F32, tag="tp")
+            word_transposes(xt, wa_sb[a][:].bitcast(F32))
+            dst = wa_grp[:, :, a * P:(a + 1) * P, :]
+            if a < 2:
+                nc.scalar.copy(out=dst, in_=xt[:].rearrange("p g u r -> p g r u"))
+            else:
+                nc.vector.tensor_copy(out=dst, in_=xt[:].rearrange("p g u r -> p g r u"))
+        nc.scalar.activation(out=tab[:].rearrange("p a s i -> p (a s i)"), in_=ang_f, func=ACT.Sin, scale=2.0 * math.pi)
+        nc.scalar.activation(out=nsin[:], in_=ang[:, 0], func=ACT.Sin, scale=-2.0 * math.pi)
+        for g in range(2):
+            nc.vector.quantize_mx(out=wa_c[:, g, :].bitcast(FP8X4), scales=wa_s[:, g, :],
+                                  in_=wa_grp[:, g].rearrange("p n u -> p (n u)").bitcast(BF16))
+
+        warm = const.tile([P, 1], F32, name="warm")
+
+        wb_grp = const.tile([P, 512, 2], F32, name="wb_grp", align_bytes=64)
+        wb_c = const.tile([P, 512], U32, name="wb_c", align_bytes=64)
+        wb_s = const.tile([P, 512], U8, name="wb_s", align_bytes=64)
+
+        def prep_wb(a2):
+            xt = tpp.tile([P, 2, 2, P], F32, tag="tp")
+            for a in range(2):
+                words = wb_sb[:, 2 * a2 + a, :].bitcast(F32).rearrange("p (w u) -> p w u", u=2)
+                for u in range(2):
+                    nc.tensor.transpose(xt[:, a, u, :], words[:, :, u], ident_f[:])
+            nc.scalar.copy(out=wb_grp[:, a2 * 256:(a2 + 1) * 256, :].rearrange("p (a r) u -> p a r u", a=2),
+                           in_=xt[:].rearrange("p a u r -> p a r u"))
+
+        def quant_wb():
+            nc.vector.quantize_mx(out=wb_c[:].bitcast(FP8X4), scales=wb_s[:],
+                                  in_=wb_grp[:].rearrange("p n u -> p (n u)").bitcast(BF16))
+
+        xtd = {}
+        grp = {}
+        hcode = {}
+        ck = {}
+        rstd = {}
+        ssq = {}
+        ckn = {}
+        ytd = {}
+        g2 = {}
+        c2 = {}
+        kv = {}
+        key_sb = {}
+        v_sb = {}
+
+        def open_chunk(c):
+            key_sb[c] = outp.tile([P, 2, 4, 192], F32, tag="key", name="key")
+            v_sb[c] = outp.tile([P, 2, 4, P], F32, tag="v", name="v")
+            cs = c % 4
+            for e in range(2):
+                x = kpe[:, c, e * P:(e + 1) * P].rearrange("p (j h i) -> p j h i", h=2, i=32)
+                rows = slice(4 * cs + 2 * e, 4 * cs + 2 * e + 2)
+                js = slice(2 * e, 2 * e + 2)
+                ra = work.tile([P, 2, 2, 32], F32, tag="ra", name="ra")
+                rb = work.tile([P, 2, 2, 32], F32, tag="rb", name="rb")
+                nc.gpsimd.tensor_tensor(out=ra[:], in0=x, in1=tab[:, 1, rows, :].unsqueeze(2).to_broadcast([P, 2, 2, 32]), op=ALU.mult)
+                nc.gpsimd.tensor_tensor(out=rb[:, :, 0, :], in0=x[:, :, 1, :], in1=nsin[:, rows, :], op=ALU.mult)
+                nc.gpsimd.tensor_tensor(out=rb[:, :, 1, :], in0=x[:, :, 0, :], in1=tab[:, 0, rows, :], op=ALU.mult)
+                nc.gpsimd.tensor_tensor(out=key_sb[c][:, 0, js, 128:192], in0=ra[:].rearrange("p j h i -> p j (h i)"),
+                                        in1=rb[:].rearrange("p j h i -> p j (h i)"), op=ALU.add)
+                nc.gpsimd.tensor_scalar(out=key_sb[c][:, 1, js, 128:192], in0=key_sb[c][:, 0, js, 128:192],
+                                        scalar1=1.0, scalar2=0.0, op0=ALU.mult, op1=ALU.add)
+
+        def t1(k):
+            xt = tpp.tile([P, 2, 2, P], F32, tag="tp")
+            word_transposes(xt, hs_sb[k // 2][:, k % 2, :].bitcast(F32))
+            xtd[k] = xt
+
+        def pass1(k):
+            grp[k] = work.tile([P, 2, P, 2], F32, tag="grp", name="grp", align_bytes=64)
+            if k < 2:
+                nc.scalar.copy(out=grp[k][:], in_=xtd[k][:].rearrange("p g u r -> p g r u"))
+            else:
+                nc.vector.tensor_copy(out=grp[k][:], in_=xtd[k][:].rearrange("p g u r -> p g r u"))
+
+        def quant_hs(k):
+            hc = work.tile([P, 256], U32, tag="hc", name="hc", align_bytes=64)
+            hsc = work.tile([P, 256], U8, tag="hsc", name="hsc", align_bytes=64)
+            nc.vector.quantize_mx(out=hc[:].bitcast(FP8X4), scales=hsc[:],
+                                  in_=grp[k][:].rearrange("p g r u -> p (g r u)").bitcast(BF16))
+            hcode[k] = (hc, hsc)
+
+        def s1(k):
+            hc, hsc = hcode[k]
+            acc = mxp.tile([P, 512], F32, tag="mx")
+            for g in range(2):
+                nc.tensor.matmul_mx(out=acc[:], lhsT=hc[:, g * P:(g + 1) * P].bitcast(FP8X4), lhsT_scale=hsc[:, g * P:(g + 1) * P],
+                                    rhs=wa_c[:, g, :].bitcast(FP8X4), rhs_scale=wa_s[:, g, :], start=(g == 0), stop=(g == 1))
+            ck[k] = acc
+
+        def square(k):
+            ssq[k] = work.tile([P, 1], F32, tag="ssq", name="ssq")
+            junk = work.tile([P, 512], BF16, tag="junk", name="junk")
+            nc.scalar.activation(out=junk[:], in_=ck[k][:], func=ACT.Square, accum_out=ssq[k][:])
+
+        def rsqrt(k):
+            rstd[k] = work.tile([P, 1], F32, tag="rs", name="rs")
+            nc.scalar.activation(out=rstd[k][:], in_=ssq[k][:], func=ACT.Abs_reciprocal_sqrt, scale=1.0 / 512.0, bias=eps_t[:, 0:1])
+
+        def pass3(k):
+            ckn[k] = work.tile([P, 512], F32, tag="ckn", name="ckn")
+            nc.scalar.activation(out=ckn[k][:], in_=ck[k][:], func=ACT.Copy, scale=rstd[k][:, 0:1])
+
+        def t2(k):
+            yt = tpp.tile([P, 4, P], F32, tag="tp")
+            for a in range(4):
+                nc.tensor.transpose(yt[:, a, :], ckn[k][:, a * P:(a + 1) * P], ident_f[:])
+            ytd[k] = yt
+
+        def pass4(k):
+            g2[k] = work.tile([P, P, 4], BF16, tag="g2", name="g2", align_bytes=64)
+            nc.vector.tensor_tensor(out=g2[k][:], in0=ytd[k][:].rearrange("p t r -> p r t"),
+                                    in1=w_pt[:].unsqueeze(1).to_broadcast([P, P, 4]), op=ALU.mult)
+
+        def quant2(k):
+            cc = work.tile([P, P], U32, tag="cc", name="cc", align_bytes=64)
+            csc = work.tile([P, P], U8, tag="csc", name="csc", align_bytes=64)
+            nc.vector.quantize_mx(out=cc[:].bitcast(FP8X4), scales=csc[:], in_=g2[k][:].rearrange("p r t -> p (r t)"))
+            c2[k] = (cc, csc)
+
+        def s2(k):
+            cc, csc = c2[k]
+            acc = mxp.tile([P, 512], F32, tag="mx")
+            nc.tensor.matmul_mx(out=acc[:], lhsT=cc[:].bitcast(FP8X4), lhsT_scale=csc[:],
+                                rhs=wb_c[:].bitcast(FP8X4), rhs_scale=wb_s[:], start=True, stop=True)
+            kv[k] = acc
+
+        def pass5(k):
+            c, j = divmod(k, 4)
+            src = kv[k][:].rearrange("p (h e d) -> p h e d", h=2, e=2)
+            if k % 8 == 7:
+                nc.vector.tensor_copy(out=key_sb[c][:, :, j, 0:P], in_=src[:, :, 0, :])
+                nc.vector.tensor_copy(out=v_sb[c][:, :, j, :], in_=src[:, :, 1, :])
+            else:
+                nc.scalar.copy(out=key_sb[c][:, :, j, 0:P], in_=src[:, :, 0, :])
+                nc.scalar.copy(out=v_sb[c][:, :, j, :], in_=src[:, :, 1, :])
+            b, cs = divmod(c, 4)
+            rows = slice(cs * 512, (cs + 1) * 512)
+            if c == 7:
+                nc.sync.dma_start(out=out_0[b, :, rows, :].rearrange("h (p j) d -> j p h d", j=4)[j], in_=key_sb[c][:, :, j, :])
+                nc.sync.dma_start(out=out_1[b, :, rows, :].rearrange("h (p j) d -> j p h d", j=4)[j], in_=v_sb[c][:, :, j, :])
+            elif j == 3:
+                nc.sync.dma_start(out=out_0[b, :, rows, :].rearrange("h (p j) d -> p h (j d)", j=4),
+                                  in_=key_sb[c][:].rearrange("p h j d -> p h (j d)"))
+                nc.sync.dma_start(out=out_1[b, :, rows, :].rearrange("h (p j) d -> p h (j d)", j=4),
+                                  in_=v_sb[c][:].rearrange("p h j d -> p h (j d)"))
+
+        def live(k):
+            return 0 <= k < N_TILES
+
+        for r in range(N_TILES + 14):
+            if r % 4 == 0 and 0 <= r // 4 - 1 < 8:
+                open_chunk(r // 4 - 1)
+            if r == 7:
+                quant_wb()
+            if live(r - 13):
+                pass5(r - 13)
+            if live(r - 8):
+                t2(r - 8)
+            elif r == 3 or r == 4:
+                prep_wb(r - 3)
+            if live(r - 12):
+                s2(r - 12)
+            if live(r - 10):
+                quant2(r - 10)
+            if live(r - 4):
+                s1(r - 4)
+            if live(r - 3):
+                quant_hs(r - 3)
+            if live(r - 5):
+                square(r - 5)
+            if live(r - 6):
+                pass3(r - 6)
+            if live(r - 5):
+                rsqrt(r - 5)
+            if live(r):
+                t1(r)
+            if live(r - 1):
+                pass1(r - 1)
+            if r == 2:
+                nc.scalar.activation(out=warm[:], in_=eps_t[:], func=ACT.Abs_reciprocal_sqrt)
+            if live(r - 8):
+                pass4(r - 8)

@@ -18,23 +18,29 @@ ACT = mybir.ActivationFunctionType
 P = 128
 EPS = 1e-6
 THETA = 10000.0
-N_TILES = 32
+N_PAIRS = 16
 
 
 def tile_modelnew_pb_t_kernel(tc, hidden_states, kv_a_w_ckv, k_pe_raw, kv_a_ln_w, kv_b_w, out_0, out_1):
     nc = tc.nc
     with ExitStack() as ctx:
         const = ctx.enter_context(tc.tile_pool(name="const", bufs=1))
-        work = ctx.enter_context(tc.tile_pool(name="work", bufs=6))
+        work = ctx.enter_context(tc.tile_pool(name="work", bufs=3))
         outp = ctx.enter_context(tc.tile_pool(name="outp", bufs=4))
-        tpp = ctx.enter_context(tc.psum_pool(name="tpp", bufs=3))
-        mxp = ctx.enter_context(tc.psum_pool(name="mxp", bufs=5))
+        xtp = ctx.enter_context(tc.psum_pool(name="xtp", bufs=2))
+        accp = ctx.enter_context(tc.psum_pool(name="accp", bufs=3))
+        ytp = ctx.enter_context(tc.psum_pool(name="ytp", bufs=1))
+        kvp = ctx.enter_context(tc.psum_pool(name="kvp", bufs=2))
         ctx.enter_context(tc.manual_schedule())
 
         s_i = const.tile([P, 16], I32, name="s_i")
         nc.gpsimd.iota(s_i[:], pattern=[[512, 4], [1, 4]], base=0, channel_multiplier=4)
         ident_f = const.tile([P, P], F32, name="ident_f")
         make_identity(nc, ident_f[:])
+        w_row = const.tile([P, 512], BF16, name="w_row")
+        nc.gpsimd.memset(w_row[:], 0.0)
+        ones = const.tile([P, P], BF16, name="ones")
+        nc.gpsimd.memset(ones[:], 1.0)
 
         one = const.tile([P, 1], F32, name="one")
         nc.vector.memset(one[:], 1.0)
@@ -49,95 +55,93 @@ def tile_modelnew_pb_t_kernel(tc, hidden_states, kv_a_w_ckv, k_pe_raw, kv_a_ln_w
         wb_sb = const.tile([P, 4, 512], BF16, name="wb_sb")
         kpe = const.tile([P, 8, 256], BF16, name="kpe")
         hs_sb = []
-        for h2 in range(16):
-            hs_c = const.tile([P, 2, 1024], BF16, name="hs%d" % h2)
-            hs_sb.append(hs_c)
+        for q in range(N_PAIRS):
+            hs_q = const.tile([P, 2, 1024], BF16, name="hs%d" % q)
+            hs_sb.append(hs_q)
 
-        def load_hs(c):
-            for e in range(2):
-                nc.sync.dma_start(out=hs_sb[2 * c + e][:].rearrange("p j d -> p (j d)"), in_=hs_v[c][:, e * 2048:(e + 1) * 2048])
-
-        def load_first_tiles():
-            for j in range(2):
-                nc.sync.dma_start(out=hs_sb[0][:, j, :], in_=hs_v[0][:, j * 1024:(j + 1) * 1024])
-            nc.sync.dma_start(out=hs_sb[1][:].rearrange("p j d -> p (j d)"), in_=hs_v[0][:, 2048:4096])
+        def load_hs(q):
+            c, e = divmod(q, 2)
+            nc.sync.dma_start(out=hs_sb[q][:].rearrange("p j d -> p (j d)"), in_=hs_v[c][:, e * 2048:(e + 1) * 2048])
 
         wa_v = kv_a_w_ckv.rearrange("(p a) d -> a p d", a=4)
         for a in range(4):
             nc.sync.dma_start(out=wa_sb[a][:], in_=wa_v[a])
-        load_first_tiles()
-        w_pt = const.tile([P, 4], BF16, name="w_pt")
-        nc.sync.dma_start(out=w_pt[:], in_=kv_a_ln_w.rearrange("(p t) -> p t", t=4))
-        nc.sync.dma_start(out=wb_sb[:], in_=kv_b_w.rearrange("(a p) k -> p a k", p=P))
+        for j in range(2):
+            nc.sync.dma_start(out=hs_sb[0][:, j, :], in_=hs_v[0][:, j * 1024:(j + 1) * 1024])
         load_hs(1)
+        nc.sync.dma_start(out=w_row[0:1, :], in_=kv_a_ln_w.rearrange("(a n) -> a n", a=1))
+        nc.sync.dma_start(out=wb_sb[:], in_=kv_b_w.rearrange("(a p) k -> p a k", p=P))
+        load_hs(2)
+        load_hs(3)
         nc.sync.dma_start(out=kpe[:], in_=k_pe_raw.flatten_outer_dims().rearrange("(c p j) r -> p c (j r)", p=P, j=4))
-        for c in range(2, 8):
-            load_hs(c)
+        for q in range(4, N_PAIRS):
+            load_hs(q)
 
         s_f = const.tile([P, 16], F32, name="s_f")
         nc.vector.tensor_copy(out=s_f[:], in_=s_i[:])
         fr = const.tile([P, 32], F32, name="fr")
-        nc.vector.memset(fr[:, 0:1], 1.0)
+        nc.vector.tensor_scalar(out=fr[:, 0:1], in0=one[:], scalar1=1.0 / (2.0 * math.pi), scalar2=None, op0=ALU.mult)
         for m in range(5):
             n = 1 << m
             nc.vector.tensor_scalar(out=fr[:, n:2 * n], in0=fr[:, 0:n], scalar1=THETA ** (-n / 32.0), scalar2=None, op0=ALU.mult)
-        nc.vector.tensor_scalar(out=fr[:], in0=fr[:], scalar1=1.0 / (2.0 * math.pi), scalar2=None, op0=ALU.mult)
         ang = const.tile([P, 2, 16, 32], F32, name="ang")
+        ang0 = ang[:, 0].rearrange("p s i -> p (s i)")
+        ang1 = ang[:, 1].rearrange("p s i -> p (s i)")
         nc.vector.tensor_tensor(out=ang[:, 0], in0=s_f[:].unsqueeze(2).to_broadcast([P, 16, 32]),
                                 in1=fr[:].unsqueeze(1).to_broadcast([P, 16, 32]), op=ALU.mult)
-        nc.vector.tensor_scalar(out=ang[:, 1], in0=ang[:, 0], scalar1=0.25, scalar2=None, op0=ALU.add)
-        ang_f = ang[:].rearrange("p a s i -> p (a s i)")
-        q_i = const.tile([P, 1024], I32, name="q_i")
-        nc.vector.tensor_copy(out=q_i[:], in_=ang_f)
-        k_f = const.tile([P, 1024], F32, name="k_f")
-        nc.vector.tensor_copy(out=k_f[:], in_=q_i[:])
-        nc.vector.tensor_tensor(out=ang_f, in0=ang_f, in1=k_f[:], op=ALU.subtract)
+        q_i = const.tile([P, 512], I32, name="q_i")
+        nc.vector.tensor_copy(out=q_i[:], in_=ang0)
+        nc.vector.tensor_tensor(out=ang0, in0=ang0, in1=q_i[:], op=ALU.subtract)
+        past = const.tile([P, 512], F32, name="past")
+        nc.vector.tensor_scalar(out=past[:], in0=ang0, scalar1=0.25, scalar2=None, op0=ALU.is_gt)
+        nc.vector.scalar_tensor_tensor(out=ang1, in0=ang0, scalar=0.25, in1=past[:], op0=ALU.add, op1=ALU.subtract)
         eps_t = const.tile([P, 1], F32, name="eps_t")
-        nc.vector.memset(eps_t[:], 1.0)
-        nc.vector.tensor_scalar(out=eps_t[:], in0=eps_t[:], scalar1=EPS, scalar2=None, op0=ALU.mult)
+        nc.vector.tensor_scalar(out=eps_t[:], in0=one[:], scalar1=EPS, scalar2=None, op0=ALU.mult)
         tab = const.tile([P, 2, 16, 32], F32, name="tab")
         nsin = const.tile([P, 16, 32], F32, name="nsin")
-
-        def word_transposes(xt, words):
-            for g in range(2):
-                for u in range(2):
-                    nc.tensor.transpose(xt[:, g, u, :], words[:, 256 * g + u:256 * (g + 1):2], ident_f[:])
 
         wa_grp = const.tile([P, 2, 512, 2], F32, name="wa_grp", align_bytes=64)
         wa_c = const.tile([P, 2, 512], U32, name="wa_c", align_bytes=64)
         wa_s = const.tile([P, 2, 512], U8, name="wa_s", align_bytes=64)
-        for a in range(4):
-            xt = tpp.tile([P, 2, 2, P], F32, tag="tp")
-            word_transposes(xt, wa_sb[a][:].bitcast(F32))
-            dst = wa_grp[:, :, a * P:(a + 1) * P, :]
-            if a < 2:
-                nc.scalar.copy(out=dst, in_=xt[:].rearrange("p g u r -> p g r u"))
-            else:
-                nc.vector.tensor_copy(out=dst, in_=xt[:].rearrange("p g u r -> p g r u"))
-        nc.scalar.activation(out=tab[:].rearrange("p a s i -> p (a s i)"), in_=ang_f, func=ACT.Sin, scale=2.0 * math.pi)
-        nc.scalar.activation(out=nsin[:], in_=ang[:, 0], func=ACT.Sin, scale=-2.0 * math.pi)
+        for u in range(2):
+            for g in range(2):
+                xt = xtp.tile([P, 2, 2, P], F32, tag="xt")
+                for e in range(2):
+                    words = wa_sb[2 * u + e][:].bitcast(F32)
+                    for v in range(2):
+                        nc.tensor.transpose(xt[:, e, v, :], words[:, 256 * g + v:256 * (g + 1):2], ident_f[:])
+                dst = wa_grp[:, g, u * 256:(u + 1) * 256, :].rearrange("p (m e) v -> p m e v", e=2)
+                src = xt[:].rearrange("p e v m -> p m e v")
+                if g == 0:
+                    nc.scalar.copy(out=dst, in_=src)
+                else:
+                    nc.vector.tensor_copy(out=dst, in_=src)
         for g in range(2):
             nc.vector.quantize_mx(out=wa_c[:, g, :].bitcast(FP8X4), scales=wa_s[:, g, :],
-                                  in_=wa_grp[:, g].rearrange("p n u -> p (n u)").bitcast(BF16))
+                                  in_=wa_grp[:, g].rearrange("p n v -> p (n v)").bitcast(BF16))
 
-        warm = const.tile([P, 1], F32, name="warm")
-
+        w_bc = const.tile([P, 2, P, 2], BF16, name="w_bc")
         wb_grp = const.tile([P, 512, 2], F32, name="wb_grp", align_bytes=64)
         wb_c = const.tile([P, 512], U32, name="wb_c", align_bytes=64)
         wb_s = const.tile([P, 512], U8, name="wb_s", align_bytes=64)
 
+        def spread_gain():
+            ps = kvp.tile([P, 512], F32, tag="kv")
+            nc.tensor.matmul(ps[:], lhsT=ones[:], rhs=w_row[:], start=True, stop=True)
+            nc.scalar.copy(out=w_bc[:], in_=ps[:].rearrange("p (m u e) -> p u m e", u=2, e=2))
+
         def prep_wb(a2):
-            xt = tpp.tile([P, 2, 2, P], F32, tag="tp")
+            xt = kvp.tile([P, 2, 2, P], F32, tag="kv")
             for a in range(2):
-                words = wb_sb[:, 2 * a2 + a, :].bitcast(F32).rearrange("p (w u) -> p w u", u=2)
-                for u in range(2):
-                    nc.tensor.transpose(xt[:, a, u, :], words[:, :, u], ident_f[:])
-            nc.scalar.copy(out=wb_grp[:, a2 * 256:(a2 + 1) * 256, :].rearrange("p (a r) u -> p a r u", a=2),
-                           in_=xt[:].rearrange("p a u r -> p a r u"))
+                words = wb_sb[:, 2 * a2 + a, :].bitcast(F32)
+                for v in range(2):
+                    nc.tensor.transpose(xt[:, a, v, :], words[:, v:256:2], ident_f[:])
+            nc.scalar.copy(out=wb_grp[:, a2 * 256:(a2 + 1) * 256, :].rearrange("p (a r) v -> p a r v", a=2),
+                           in_=xt[:].rearrange("p a v r -> p a r v"))
 
         def quant_wb():
             nc.vector.quantize_mx(out=wb_c[:].bitcast(FP8X4), scales=wb_s[:],
-                                  in_=wb_grp[:].rearrange("p n u -> p (n u)").bitcast(BF16))
+                                  in_=wb_grp[:].rearrange("p n v -> p (n v)").bitcast(BF16))
 
         xtd = {}
         grp = {}
@@ -171,123 +175,151 @@ def tile_modelnew_pb_t_kernel(tc, hidden_states, kv_a_w_ckv, k_pe_raw, kv_a_ln_w
                 nc.gpsimd.tensor_scalar(out=key_sb[c][:, 1, js, 128:192], in0=key_sb[c][:, 0, js, 128:192],
                                         scalar1=1.0, scalar2=0.0, op0=ALU.mult, op1=ALU.add)
 
-        def t1(k):
-            xt = tpp.tile([P, 2, 2, P], F32, tag="tp")
-            word_transposes(xt, hs_sb[k // 2][:, k % 2, :].bitcast(F32))
-            xtd[k] = xt
+        def t1(q):
+            xtd[q] = []
+            for i in range(2):
+                xt = xtp.tile([P, 2, 2, P], F32, tag="xt")
+                words = hs_sb[q][:, i, :].bitcast(F32)
+                for g in range(2):
+                    for v in range(2):
+                        nc.tensor.transpose(xt[:, g, v, :], words[:, 256 * g + v:256 * (g + 1):2], ident_f[:])
+                xtd[q].append(xt)
 
-        def pass1(k):
-            grp[k] = work.tile([P, 2, P, 2], F32, tag="grp", name="grp", align_bytes=64)
-            if k < 2:
-                nc.scalar.copy(out=grp[k][:], in_=xtd[k][:].rearrange("p g u r -> p g r u"))
-            else:
-                nc.vector.tensor_copy(out=grp[k][:], in_=xtd[k][:].rearrange("p g u r -> p g r u"))
+        def pass1(q, i):
+            if i == 0:
+                grp[q] = work.tile([P, 2, 2, P, 2], F32, tag="grp", name="grp", align_bytes=64)
+            nc.vector.tensor_copy(out=grp[q][:, i], in_=xtd[q][i][:].rearrange("p g v r -> p g r v"))
 
-        def quant_hs(k):
-            hc = work.tile([P, 256], U32, tag="hc", name="hc", align_bytes=64)
-            hsc = work.tile([P, 256], U8, tag="hsc", name="hsc", align_bytes=64)
+        def quant_hs(q):
+            hc = work.tile([P, 512], U32, tag="hc", name="hc", align_bytes=64)
+            hsc = work.tile([P, 512], U8, tag="hsc", name="hsc", align_bytes=64)
             nc.vector.quantize_mx(out=hc[:].bitcast(FP8X4), scales=hsc[:],
-                                  in_=grp[k][:].rearrange("p g r u -> p (g r u)").bitcast(BF16))
-            hcode[k] = (hc, hsc)
+                                  in_=grp[q][:].rearrange("p i g r v -> p (i g r v)").bitcast(BF16))
+            hcode[q] = (hc, hsc)
 
-        def s1(k):
-            hc, hsc = hcode[k]
-            acc = mxp.tile([P, 512], F32, tag="mx")
-            for g in range(2):
-                nc.tensor.matmul_mx(out=acc[:], lhsT=hc[:, g * P:(g + 1) * P].bitcast(FP8X4), lhsT_scale=hsc[:, g * P:(g + 1) * P],
-                                    rhs=wa_c[:, g, :].bitcast(FP8X4), rhs_scale=wa_s[:, g, :], start=(g == 0), stop=(g == 1))
-            ck[k] = acc
+        def s1(q):
+            hc, hsc = hcode[q]
+            ck[q] = []
+            for i in range(2):
+                acc = accp.tile([P, 512], F32, tag="acc")
+                for g in range(2):
+                    cols = slice((2 * i + g) * P, (2 * i + g + 1) * P)
+                    nc.tensor.matmul_mx(out=acc[:], lhsT=hc[:, cols].bitcast(FP8X4), lhsT_scale=hsc[:, cols],
+                                        rhs=wa_c[:, g, :].bitcast(FP8X4), rhs_scale=wa_s[:, g, :], start=(g == 0), stop=(g == 1))
+                ck[q].append(acc)
 
-        def square(k):
-            ssq[k] = work.tile([P, 1], F32, tag="ssq", name="ssq")
+        def square(q, i):
+            if i == 0:
+                ssq[q] = work.tile([P, 2], F32, tag="ssq", name="ssq")
+                rstd[q] = work.tile([P, 2], F32, tag="rs", name="rs")
             junk = work.tile([P, 512], BF16, tag="junk", name="junk")
-            nc.scalar.activation(out=junk[:], in_=ck[k][:], func=ACT.Square, accum_out=ssq[k][:])
+            nc.scalar.activation(out=junk[:], in_=ck[q][i][:], func=ACT.Square, accum_out=ssq[q][:, i:i + 1])
 
-        def rsqrt(k):
-            rstd[k] = work.tile([P, 1], F32, tag="rs", name="rs")
-            nc.scalar.activation(out=rstd[k][:], in_=ssq[k][:], func=ACT.Abs_reciprocal_sqrt, scale=1.0 / 512.0, bias=eps_t[:, 0:1])
+        def rsqrt(q, i):
+            nc.scalar.activation(out=rstd[q][:, i:i + 1], in_=ssq[q][:, i:i + 1], func=ACT.Abs_reciprocal_sqrt,
+                                 scale=1.0 / 512.0, bias=eps_t[:, 0:1])
 
-        def pass3(k):
-            ckn[k] = work.tile([P, 512], F32, tag="ckn", name="ckn")
-            nc.scalar.activation(out=ckn[k][:], in_=ck[k][:], func=ACT.Copy, scale=rstd[k][:, 0:1])
+        def normalise(q, i):
+            if i == 0:
+                ckn[q] = work.tile([P, 2, 512], BF16, tag="ckn", name="ckn")
+            nc.vector.scalar_tensor_tensor(out=ckn[q][:, i, :], in0=ck[q][i][:], scalar=rstd[q][:, i:i + 1],
+                                           in1=w_bc[:].rearrange("p u m e -> p (u m e)"), op0=ALU.mult, op1=ALU.mult)
 
-        def t2(k):
-            yt = tpp.tile([P, 4, P], F32, tag="tp")
-            for a in range(4):
-                nc.tensor.transpose(yt[:, a, :], ckn[k][:, a * P:(a + 1) * P], ident_f[:])
-            ytd[k] = yt
+        def t2(q):
+            yt = ytp.tile([P, 2, 2, P], F32, tag="yt")
+            for i in range(2):
+                words = ckn[q][:, i, :].bitcast(F32)
+                for u in range(2):
+                    nc.tensor.transpose(yt[:, i, u, :], words[:, u * P:(u + 1) * P], ident_f[:])
+            ytd[q] = yt
 
-        def pass4(k):
-            g2[k] = work.tile([P, P, 4], BF16, tag="g2", name="g2", align_bytes=64)
-            nc.vector.tensor_tensor(out=g2[k][:], in0=ytd[k][:].rearrange("p t r -> p r t"),
-                                    in1=w_pt[:].unsqueeze(1).to_broadcast([P, P, 4]), op=ALU.mult)
+        def pass4(q):
+            g2[q] = work.tile([P, 2, P, 2], F32, tag="g2", name="g2", align_bytes=64)
+            nc.scalar.copy(out=g2[q][:], in_=ytd[q][:].rearrange("p i u r -> p i r u"))
 
-        def quant2(k):
-            cc = work.tile([P, P], U32, tag="cc", name="cc", align_bytes=64)
-            csc = work.tile([P, P], U8, tag="csc", name="csc", align_bytes=64)
-            nc.vector.quantize_mx(out=cc[:].bitcast(FP8X4), scales=csc[:], in_=g2[k][:].rearrange("p r t -> p (r t)"))
-            c2[k] = (cc, csc)
+        def quant2(q):
+            cc = work.tile([P, 256], U32, tag="cc", name="cc", align_bytes=64)
+            csc = work.tile([P, 256], U8, tag="csc", name="csc", align_bytes=64)
+            nc.vector.quantize_mx(out=cc[:].bitcast(FP8X4), scales=csc[:],
+                                  in_=g2[q][:].rearrange("p i r u -> p (i r u)").bitcast(BF16))
+            c2[q] = (cc, csc)
 
-        def s2(k):
-            cc, csc = c2[k]
-            acc = mxp.tile([P, 512], F32, tag="mx")
-            nc.tensor.matmul_mx(out=acc[:], lhsT=cc[:].bitcast(FP8X4), lhsT_scale=csc[:],
-                                rhs=wb_c[:].bitcast(FP8X4), rhs_scale=wb_s[:], start=True, stop=True)
-            kv[k] = acc
+        def s2(q):
+            cc, csc = c2[q]
+            kv[q] = []
+            for i in range(2):
+                acc = kvp.tile([P, 512], F32, tag="kv")
+                cols = slice(i * P, (i + 1) * P)
+                nc.tensor.matmul_mx(out=acc[:], lhsT=cc[:, cols].bitcast(FP8X4), lhsT_scale=csc[:, cols],
+                                    rhs=wb_c[:].bitcast(FP8X4), rhs_scale=wb_s[:], start=True, stop=True)
+                kv[q].append(acc)
 
-        def pass5(k):
-            c, j = divmod(k, 4)
-            src = kv[k][:].rearrange("p (h e d) -> p h e d", h=2, e=2)
-            if k % 8 == 7:
-                nc.vector.tensor_copy(out=key_sb[c][:, :, j, 0:P], in_=src[:, :, 0, :])
-                nc.vector.tensor_copy(out=v_sb[c][:, :, j, :], in_=src[:, :, 1, :])
-            else:
-                nc.scalar.copy(out=key_sb[c][:, :, j, 0:P], in_=src[:, :, 0, :])
-                nc.scalar.copy(out=v_sb[c][:, :, j, :], in_=src[:, :, 1, :])
+        def emit(q, i, part):
+            c, j = divmod(2 * q + i, 4)
+            src = kv[q][i][:].rearrange("p (h e d) -> p h e d", h=2, e=2)
             b, cs = divmod(c, 4)
             rows = slice(cs * 512, (cs + 1) * 512)
-            if c == 7:
-                nc.sync.dma_start(out=out_0[b, :, rows, :].rearrange("h (p j) d -> j p h d", j=4)[j], in_=key_sb[c][:, :, j, :])
-                nc.sync.dma_start(out=out_1[b, :, rows, :].rearrange("h (p j) d -> j p h d", j=4)[j], in_=v_sb[c][:, :, j, :])
-            elif j == 3:
-                nc.sync.dma_start(out=out_0[b, :, rows, :].rearrange("h (p j) d -> p h (j d)", j=4),
-                                  in_=key_sb[c][:].rearrange("p h j d -> p h (j d)"))
-                nc.sync.dma_start(out=out_1[b, :, rows, :].rearrange("h (p j) d -> p h (j d)", j=4),
-                                  in_=v_sb[c][:].rearrange("p h j d -> p h (j d)"))
+            if part == 0:
+                nc.scalar.copy(out=key_sb[c][:, :, j, 0:P], in_=src[:, :, 0, :])
+                if c == 7:
+                    nc.sync.dma_start(out=out_0[b, :, rows, :].rearrange("h (p j) d -> j p h d", j=4)[j], in_=key_sb[c][:, :, j, :])
+                elif j == 3:
+                    nc.sync.dma_start(out=out_0[b, :, rows, :].rearrange("h (p j) d -> p h (j d)", j=4),
+                                      in_=key_sb[c][:].rearrange("p h j d -> p h (j d)"))
+            else:
+                nc.scalar.copy(out=v_sb[c][:, :, j, :], in_=src[:, :, 1, :])
+                if c == 7:
+                    nc.sync.dma_start(out=out_1[b, :, rows, :].rearrange("h (p j) d -> j p h d", j=4)[j], in_=v_sb[c][:, :, j, :])
+                elif j == 3:
+                    nc.sync.dma_start(out=out_1[b, :, rows, :].rearrange("h (p j) d -> p h (j d)", j=4),
+                                      in_=v_sb[c][:].rearrange("p h j d -> p h (j d)"))
 
-        def live(k):
-            return 0 <= k < N_TILES
+        def live(q):
+            return 0 <= q < N_PAIRS
 
-        for r in range(N_TILES + 14):
-            if r % 4 == 0 and 0 <= r // 4 - 1 < 8:
-                open_chunk(r // 4 - 1)
-            if r == 7:
-                quant_wb()
-            if live(r - 13):
-                pass5(r - 13)
-            if live(r - 8):
-                t2(r - 8)
-            elif r == 3 or r == 4:
-                prep_wb(r - 3)
-            if live(r - 12):
-                s2(r - 12)
-            if live(r - 10):
-                quant2(r - 10)
-            if live(r - 4):
-                s1(r - 4)
-            if live(r - 3):
-                quant_hs(r - 3)
-            if live(r - 5):
-                square(r - 5)
-            if live(r - 6):
-                pass3(r - 6)
-            if live(r - 5):
-                rsqrt(r - 5)
+        nc.scalar.activation(out=tab[:].rearrange("p a s i -> p (a s i)"), in_=ang[:].rearrange("p a s i -> p (a s i)"),
+                             func=ACT.Sin, scale=2.0 * math.pi)
+        nc.scalar.activation(out=nsin[:], in_=ang[:, 0], func=ACT.Sin, scale=-2.0 * math.pi)
+        warm = const.tile([P, 1], F32, name="warm")
+        nc.scalar.activation(out=warm[:], in_=eps_t[:], func=ACT.Abs_reciprocal_sqrt)
+
+        for r in range(N_PAIRS + 4):
+            if r % 2 == 1 and r // 2 < 8:
+                open_chunk(r // 2)
             if live(r):
                 t1(r)
-            if live(r - 1):
-                pass1(r - 1)
+            if r == 0:
+                spread_gain()
+            if r == 1:
+                prep_wb(0)
+                prep_wb(1)
+            if live(r - 2):
+                t2(r - 2)
+            if live(r):
+                pass1(r, 0)
+                pass1(r, 1)
+            if live(r - 2):
+                pass4(r - 2)
             if r == 2:
-                nc.scalar.activation(out=warm[:], in_=eps_t[:], func=ACT.Abs_reciprocal_sqrt)
-            if live(r - 8):
-                pass4(r - 8)
+                quant_wb()
+            if live(r - 2):
+                quant2(r - 2)
+            if live(r):
+                quant_hs(r)
+            if live(r - 1):
+                s1(r - 1)
+            if live(r - 3):
+                s2(r - 3)
+            if live(r - 1):
+                square(r - 1, 0)
+                rsqrt(r - 1, 0)
+                square(r - 1, 1)
+                rsqrt(r - 1, 1)
+            if live(r - 3):
+                emit(r - 3, 0, 0)
+                emit(r - 3, 0, 1)
+                emit(r - 3, 1, 0)
+                emit(r - 3, 1, 1)
+            if live(r - 1):
+                normalise(r - 1, 0)
+                normalise(r - 1, 1)

@@ -84,28 +84,34 @@ def tile_modelnew_pb_t_kernel(tc, hidden_states, kv_a_w_ckv, k_pe_raw, kv_a_ln_w
         for m in range(5):
             n = 1 << m
             nc.vector.tensor_scalar(out=fr[:, n:2 * n], in0=fr[:, 0:n], scalar1=THETA ** (-n / 32.0), scalar2=None, op0=ALU.mult)
-        ang = const.tile([P, 2, 16, 32], F32, name="ang")
-        ang0 = ang[:, 0].rearrange("p s i -> p (s i)")
-        ang1 = ang[:, 1].rearrange("p s i -> p (s i)")
-        nc.vector.tensor_tensor(out=ang[:, 0], in0=s_f[:].unsqueeze(2).to_broadcast([P, 16, 32]),
+        ang = const.tile([P, 16, 32], F32, name="ang")
+        ang_f = ang[:].rearrange("p s i -> p (s i)")
+        nc.vector.tensor_tensor(out=ang[:], in0=s_f[:].unsqueeze(2).to_broadcast([P, 16, 32]),
                                 in1=fr[:].unsqueeze(1).to_broadcast([P, 16, 32]), op=ALU.mult)
         q_i = const.tile([P, 512], I32, name="q_i")
-        nc.vector.tensor_copy(out=q_i[:], in_=ang0)
-        nc.vector.tensor_tensor(out=ang0, in0=ang0, in1=q_i[:], op=ALU.subtract)
-        past = const.tile([P, 512], F32, name="past")
-        nc.vector.tensor_scalar(out=past[:], in0=ang0, scalar1=0.25, scalar2=None, op0=ALU.is_gt)
-        nc.vector.scalar_tensor_tensor(out=ang1, in0=ang0, scalar=0.25, in1=past[:], op0=ALU.add, op1=ALU.subtract)
+        nc.vector.tensor_copy(out=q_i[:], in_=ang_f)
+        nc.vector.tensor_tensor(out=ang_f, in0=ang_f, in1=q_i[:], op=ALU.subtract)
+        ang_abs = const.tile([P, 512], F32, name="ang_abs")
+        nc.vector.scalar_tensor_tensor(out=ang_abs[:], in0=ang_f, scalar=-1.0, in1=ang_f, op0=ALU.mult, op1=ALU.max)
+        quarter = const.tile([P, 1], F32, name="quarter")
+        nc.vector.tensor_scalar(out=quarter[:], in0=one[:], scalar1=math.pi / 2.0, scalar2=None, op0=ALU.mult)
         eps_t = const.tile([P, 1], F32, name="eps_t")
         nc.vector.tensor_scalar(out=eps_t[:], in0=one[:], scalar1=EPS, scalar2=None, op0=ALU.mult)
-        tab = const.tile([P, 2, 16, 32], F32, name="tab")
-        nsin = const.tile([P, 16, 32], F32, name="nsin")
+        sin_t = const.tile([P, 16, 32], F32, name="sin_t")
+        cos_t = const.tile([P, 16, 32], F32, name="cos_t")
+        nc.scalar.activation(out=sin_t[:], in_=ang[:], func=ACT.Sin, scale=2.0 * math.pi)
+        nc.scalar.activation(out=cos_t[:].rearrange("p s i -> p (s i)"), in_=ang_abs[:], func=ACT.Sin, scale=-2.0 * math.pi, bias=quarter[:, 0:1])
+        warm = const.tile([P, 1], F32, name="warm")
 
         wa_grp = const.tile([P, 2, 512, 2], F32, name="wa_grp", align_bytes=64)
         wa_c = const.tile([P, 2, 512], U32, name="wa_c", align_bytes=64)
         wa_s = const.tile([P, 2, 512], U8, name="wa_s", align_bytes=64)
         for u in range(2):
             for g in range(2):
-                xt = xtp.tile([P, 2, 2, P], F32, tag="xt")
+                if 2 * u + g < 3:
+                    xt = accp.tile([P, 2, 2, P], F32, tag="acc")
+                else:
+                    xt = kvp.tile([P, 2, 2, P], F32, tag="kv")
                 for e in range(2):
                     words = wa_sb[2 * u + e][:].bitcast(F32)
                     for v in range(2):
@@ -126,7 +132,7 @@ def tile_modelnew_pb_t_kernel(tc, hidden_states, kv_a_w_ckv, k_pe_raw, kv_a_ln_w
         wb_s = const.tile([P, 512], U8, name="wb_s", align_bytes=64)
 
         def spread_gain():
-            ps = kvp.tile([P, 512], F32, tag="kv")
+            ps = ytp.tile([P, 512], F32, tag="yt")
             nc.tensor.matmul(ps[:], lhsT=ones[:], rhs=w_row[:], start=True, stop=True)
             nc.scalar.copy(out=w_bc[:], in_=ps[:].rearrange("p (m u e) -> p u m e", u=2, e=2))
 
@@ -167,11 +173,10 @@ def tile_modelnew_pb_t_kernel(tc, hidden_states, kv_a_w_ckv, k_pe_raw, kv_a_ln_w
                 js = slice(2 * e, 2 * e + 2)
                 ra = work.tile([P, 2, 2, 32], F32, tag="ra", name="ra")
                 rb = work.tile([P, 2, 2, 32], F32, tag="rb", name="rb")
-                nc.gpsimd.tensor_tensor(out=ra[:], in0=x, in1=tab[:, 1, rows, :].unsqueeze(2).to_broadcast([P, 2, 2, 32]), op=ALU.mult)
-                nc.gpsimd.tensor_tensor(out=rb[:, :, 0, :], in0=x[:, :, 1, :], in1=nsin[:, rows, :], op=ALU.mult)
-                nc.gpsimd.tensor_tensor(out=rb[:, :, 1, :], in0=x[:, :, 0, :], in1=tab[:, 0, rows, :], op=ALU.mult)
-                nc.gpsimd.tensor_tensor(out=key_sb[c][:, 0, js, 128:192], in0=ra[:].rearrange("p j h i -> p j (h i)"),
-                                        in1=rb[:].rearrange("p j h i -> p j (h i)"), op=ALU.add)
+                nc.gpsimd.tensor_tensor(out=ra[:], in0=x, in1=cos_t[:, rows, :].unsqueeze(2).to_broadcast([P, 2, 2, 32]), op=ALU.mult)
+                nc.gpsimd.tensor_tensor(out=rb[:], in0=x, in1=sin_t[:, rows, :].unsqueeze(2).to_broadcast([P, 2, 2, 32]), op=ALU.mult)
+                nc.gpsimd.tensor_tensor(out=key_sb[c][:, 0, js, 128:160], in0=ra[:, :, 0, :], in1=rb[:, :, 1, :], op=ALU.subtract)
+                nc.gpsimd.tensor_tensor(out=key_sb[c][:, 0, js, 160:192], in0=ra[:, :, 1, :], in1=rb[:, :, 0, :], op=ALU.add)
                 nc.gpsimd.tensor_scalar(out=key_sb[c][:, 1, js, 128:192], in0=key_sb[c][:, 0, js, 128:192],
                                         scalar1=1.0, scalar2=0.0, op0=ALU.mult, op1=ALU.add)
 
@@ -188,7 +193,11 @@ def tile_modelnew_pb_t_kernel(tc, hidden_states, kv_a_w_ckv, k_pe_raw, kv_a_ln_w
         def pass1(q, i):
             if i == 0:
                 grp[q] = work.tile([P, 2, 2, P, 2], F32, tag="grp", name="grp", align_bytes=64)
-            nc.vector.tensor_copy(out=grp[q][:, i], in_=xtd[q][i][:].rearrange("p g v r -> p g r v"))
+            src = xtd[q][i][:].rearrange("p g v r -> p g r v")
+            if q == 0:
+                nc.scalar.copy(out=grp[q][:, i], in_=src)
+            else:
+                nc.vector.tensor_copy(out=grp[q][:, i], in_=src)
 
         def quant_hs(q):
             hc = work.tile([P, 512], U32, tag="hc", name="hc", align_bytes=64)
@@ -215,8 +224,8 @@ def tile_modelnew_pb_t_kernel(tc, hidden_states, kv_a_w_ckv, k_pe_raw, kv_a_ln_w
             junk = work.tile([P, 512], BF16, tag="junk", name="junk")
             nc.scalar.activation(out=junk[:], in_=ck[q][i][:], func=ACT.Square, accum_out=ssq[q][:, i:i + 1])
 
-        def rsqrt(q, i):
-            nc.scalar.activation(out=rstd[q][:, i:i + 1], in_=ssq[q][:, i:i + 1], func=ACT.Abs_reciprocal_sqrt,
+        def rsqrt(q):
+            nc.scalar.activation(out=rstd[q][:], in_=ssq[q][:], func=ACT.Abs_reciprocal_sqrt,
                                  scale=1.0 / 512.0, bias=eps_t[:, 0:1])
 
         def normalise(q, i):
@@ -233,16 +242,26 @@ def tile_modelnew_pb_t_kernel(tc, hidden_states, kv_a_w_ckv, k_pe_raw, kv_a_ln_w
                     nc.tensor.transpose(yt[:, i, u, :], words[:, u * P:(u + 1) * P], ident_f[:])
             ytd[q] = yt
 
-        def pass4(q):
-            g2[q] = work.tile([P, 2, P, 2], F32, tag="g2", name="g2", align_bytes=64)
-            nc.scalar.copy(out=g2[q][:], in_=ytd[q][:].rearrange("p i u r -> p i r u"))
+        def pass4(q, i=None):
+            if not i:
+                g2[q] = work.tile([P, 2, P, 2], F32, tag="g2", name="g2", align_bytes=64)
+            s = slice(0, 2) if i is None else slice(i, i + 1)
+            src = ytd[q][:, s].rearrange("p i u r -> p i r u")
+            if i == 0:
+                nc.vector.tensor_copy(out=g2[q][:, s], in_=src)
+            else:
+                nc.scalar.copy(out=g2[q][:, s], in_=src)
 
-        def quant2(q):
-            cc = work.tile([P, 256], U32, tag="cc", name="cc", align_bytes=64)
-            csc = work.tile([P, 256], U8, tag="csc", name="csc", align_bytes=64)
-            nc.vector.quantize_mx(out=cc[:].bitcast(FP8X4), scales=csc[:],
-                                  in_=g2[q][:].rearrange("p i r u -> p (i r u)").bitcast(BF16))
-            c2[q] = (cc, csc)
+        def quant2(q, i=None):
+            if not i:
+                cc = work.tile([P, 256], U32, tag="cc", name="cc", align_bytes=64)
+                csc = work.tile([P, 256], U8, tag="csc", name="csc", align_bytes=64)
+                c2[q] = (cc, csc)
+            cc, csc = c2[q]
+            s = slice(0, 2) if i is None else slice(i, i + 1)
+            cols = slice(0, 256) if i is None else slice(i * P, (i + 1) * P)
+            nc.vector.quantize_mx(out=cc[:, cols].bitcast(FP8X4), scales=csc[:, cols],
+                                  in_=g2[q][:, s].rearrange("p i r u -> p (i r u)").bitcast(BF16))
 
         def s2(q):
             cc, csc = c2[q]
@@ -256,70 +275,85 @@ def tile_modelnew_pb_t_kernel(tc, hidden_states, kv_a_w_ckv, k_pe_raw, kv_a_ln_w
 
         def emit(q, i, part):
             c, j = divmod(2 * q + i, 4)
-            src = kv[q][i][:].rearrange("p (h e d) -> p h e d", h=2, e=2)
+            src = kv[q][i][:].rearrange("p (h e d) -> p h e d", h=2, e=2)[:, :, part, :]
+            dst = key_sb[c][:, :, j, 0:P] if part == 0 else v_sb[c][:, :, j, :]
+            if q >= N_PAIRS - 3 and i == 0:
+                nc.vector.tensor_copy(out=dst, in_=src)
+            else:
+                nc.scalar.copy(out=dst, in_=src)
+
+        def store(q, i, part):
+            c, j = divmod(2 * q + i, 4)
             b, cs = divmod(c, 4)
             rows = slice(cs * 512, (cs + 1) * 512)
-            if part == 0:
-                nc.scalar.copy(out=key_sb[c][:, :, j, 0:P], in_=src[:, :, 0, :])
-                if c == 7:
-                    nc.sync.dma_start(out=out_0[b, :, rows, :].rearrange("h (p j) d -> j p h d", j=4)[j], in_=key_sb[c][:, :, j, :])
-                elif j == 3:
-                    nc.sync.dma_start(out=out_0[b, :, rows, :].rearrange("h (p j) d -> p h (j d)", j=4),
-                                      in_=key_sb[c][:].rearrange("p h j d -> p h (j d)"))
+            if q == N_PAIRS - 1:
+                js = slice(j, j + 1)
+            elif c >= 6 and i == 1:
+                js = slice(j - 1, j + 1)
+            elif j == 3:
+                js = slice(0, 4)
             else:
-                nc.scalar.copy(out=v_sb[c][:, :, j, :], in_=src[:, :, 1, :])
-                if c == 7:
-                    nc.sync.dma_start(out=out_1[b, :, rows, :].rearrange("h (p j) d -> j p h d", j=4)[j], in_=v_sb[c][:, :, j, :])
-                elif j == 3:
-                    nc.sync.dma_start(out=out_1[b, :, rows, :].rearrange("h (p j) d -> p h (j d)", j=4),
-                                      in_=v_sb[c][:].rearrange("p h j d -> p h (j d)"))
+                return
+            out = out_0 if part == 0 else out_1
+            tile = key_sb[c] if part == 0 else v_sb[c]
+            view = out[b, :, rows, :].rearrange("h (p j) d -> p h j d", j=4)
+            if j == 3 and js.start == 0:
+                nc.sync.dma_start(out=view.rearrange("p h j d -> p h (j d)"), in_=tile[:].rearrange("p h j d -> p h (j d)"))
+            else:
+                nc.sync.dma_start(out=view[:, :, js, :], in_=tile[:, :, js, :])
 
         def live(q):
             return 0 <= q < N_PAIRS
 
-        nc.scalar.activation(out=tab[:].rearrange("p a s i -> p (a s i)"), in_=ang[:].rearrange("p a s i -> p (a s i)"),
-                             func=ACT.Sin, scale=2.0 * math.pi)
-        nc.scalar.activation(out=nsin[:], in_=ang[:, 0], func=ACT.Sin, scale=-2.0 * math.pi)
-        warm = const.tile([P, 1], F32, name="warm")
-        nc.scalar.activation(out=warm[:], in_=eps_t[:], func=ACT.Abs_reciprocal_sqrt)
-
-        for r in range(N_PAIRS + 4):
+        for r in range(N_PAIRS + 5):
             if r % 2 == 1 and r // 2 < 8:
                 open_chunk(r // 2)
             if live(r):
                 t1(r)
-            if r == 0:
-                spread_gain()
             if r == 1:
+                spread_gain()
+            if r == 2:
                 prep_wb(0)
                 prep_wb(1)
-            if live(r - 2):
-                t2(r - 2)
+            if live(r - 3):
+                t2(r - 3)
             if live(r):
                 pass1(r, 0)
                 pass1(r, 1)
-            if live(r - 2):
-                pass4(r - 2)
-            if r == 2:
+            if r == 0:
+                nc.scalar.activation(out=warm[:], in_=eps_t[:], func=ACT.Abs_reciprocal_sqrt)
+            if r - 3 == N_PAIRS - 1:
+                pass4(r - 3, 0)
+                pass4(r - 3, 1)
+            elif live(r - 3):
+                pass4(r - 3)
+            if r == 3:
                 quant_wb()
-            if live(r - 2):
-                quant2(r - 2)
+            if r - 3 == N_PAIRS - 1:
+                quant2(r - 3, 0)
+                quant2(r - 3, 1)
+            elif live(r - 3):
+                quant2(r - 3)
             if live(r):
                 quant_hs(r)
             if live(r - 1):
                 s1(r - 1)
-            if live(r - 3):
-                s2(r - 3)
+            if live(r - 4):
+                s2(r - 4)
             if live(r - 1):
                 square(r - 1, 0)
-                rsqrt(r - 1, 0)
+            if live(r - 1):
                 square(r - 1, 1)
-                rsqrt(r - 1, 1)
-            if live(r - 3):
-                emit(r - 3, 0, 0)
-                emit(r - 3, 0, 1)
-                emit(r - 3, 1, 0)
-                emit(r - 3, 1, 1)
+            if live(r - 4):
+                for part in range(2):
+                    emit(r - 4, 0, part)
+                    store(r - 4, 0, part)
+            if live(r - 1):
+                rsqrt(r - 1)
+            if live(r - 4):
+                for part in range(2):
+                    emit(r - 4, 1, part)
+                    store(r - 4, 1, part)
             if live(r - 1):
                 normalise(r - 1, 0)
                 normalise(r - 1, 1)

@@ -194,7 +194,7 @@ def tile_modelnew_pb_t_kernel(tc, hidden_states, kv_a_w_ckv, k_pe_raw, kv_a_ln_w
             if i == 0:
                 grp[q] = work.tile([P, 2, 2, P, 2], F32, tag="grp", name="grp", align_bytes=64)
             src = xtd[q][i][:].rearrange("p g v r -> p g r v")
-            if q == 0:
+            if q == 0 or (i == 1 and q % 4 == 3):
                 nc.scalar.copy(out=grp[q][:, i], in_=src)
             else:
                 nc.vector.tensor_copy(out=grp[q][:, i], in_=src)
@@ -224,8 +224,8 @@ def tile_modelnew_pb_t_kernel(tc, hidden_states, kv_a_w_ckv, k_pe_raw, kv_a_ln_w
             junk = work.tile([P, 512], BF16, tag="junk", name="junk")
             nc.scalar.activation(out=junk[:], in_=ck[q][i][:], func=ACT.Square, accum_out=ssq[q][:, i:i + 1])
 
-        def rsqrt(q):
-            nc.scalar.activation(out=rstd[q][:], in_=ssq[q][:], func=ACT.Abs_reciprocal_sqrt,
+        def rsqrt(q, i):
+            nc.scalar.activation(out=rstd[q][:, i:i + 1], in_=ssq[q][:, i:i + 1], func=ACT.Abs_reciprocal_sqrt,
                                  scale=1.0 / 512.0, bias=eps_t[:, 0:1])
 
         def normalise(q, i):
@@ -344,16 +344,19 @@ def tile_modelnew_pb_t_kernel(tc, hidden_states, kv_a_w_ckv, k_pe_raw, kv_a_ln_w
                 square(r - 1, 0)
             if live(r - 1):
                 square(r - 1, 1)
+            if live(r - 1):
+                rsqrt(r - 1, 0)
             if live(r - 4):
                 for part in range(2):
                     emit(r - 4, 0, part)
                     store(r - 4, 0, part)
             if live(r - 1):
-                rsqrt(r - 1)
+                rsqrt(r - 1, 1)
             if live(r - 4):
                 for part in range(2):
                     emit(r - 4, 1, part)
                     store(r - 4, 1, part)
             if live(r - 1):
                 normalise(r - 1, 0)
+            if live(r - 1):
                 normalise(r - 1, 1)

@@ -68,8 +68,8 @@ def tile_modelnew_pb_t_kernel(tc, hidden_states, kv_a_w_ckv, k_pe_raw, kv_a_ln_w
             nc.sync.dma_start(out=wa_sb[a][:], in_=wa_v[a])
         for j in range(2):
             nc.sync.dma_start(out=hs_sb[0][:, j, :], in_=hs_v[0][:, j * 1024:(j + 1) * 1024])
-        load_hs(1)
         nc.sync.dma_start(out=w_row[0:1, :], in_=kv_a_ln_w.rearrange("(a n) -> a n", a=1))
+        load_hs(1)
         nc.sync.dma_start(out=wb_sb[:], in_=kv_b_w.rearrange("(a p) k -> p a k", p=P))
         load_hs(2)
         load_hs(3)
@@ -80,23 +80,29 @@ def tile_modelnew_pb_t_kernel(tc, hidden_states, kv_a_w_ckv, k_pe_raw, kv_a_ln_w
         s_f = const.tile([P, 16], F32, name="s_f")
         nc.vector.tensor_copy(out=s_f[:], in_=s_i[:])
         fr = const.tile([P, 32], F32, name="fr")
-        nc.vector.tensor_scalar(out=fr[:, 0:1], in0=one[:], scalar1=1.0 / (2.0 * math.pi), scalar2=None, op0=ALU.mult)
-        for m in range(5):
-            n = 1 << m
+        for i in range(4):
+            nc.vector.tensor_scalar(out=fr[:, i:i + 1], in0=one[:], scalar1=THETA ** (-i / 32.0) / (2.0 * math.pi), scalar2=None, op0=ALU.mult)
+        eps_t = const.tile([P, 1], F32, name="eps_t")
+        nc.vector.tensor_scalar(out=eps_t[:], in0=one[:], scalar1=EPS, scalar2=None, op0=ALU.mult)
+        quarter = const.tile([P, 1], F32, name="quarter")
+        nc.vector.tensor_scalar(out=quarter[:], in0=one[:], scalar1=math.pi / 2.0, scalar2=None, op0=ALU.mult)
+        for n in (4, 8, 16):
             nc.vector.tensor_scalar(out=fr[:, n:2 * n], in0=fr[:, 0:n], scalar1=THETA ** (-n / 32.0), scalar2=None, op0=ALU.mult)
         ang = const.tile([P, 16, 32], F32, name="ang")
         ang_f = ang[:].rearrange("p s i -> p (s i)")
-        nc.vector.tensor_tensor(out=ang[:], in0=s_f[:].unsqueeze(2).to_broadcast([P, 16, 32]),
-                                in1=fr[:].unsqueeze(1).to_broadcast([P, 16, 32]), op=ALU.mult)
         q_i = const.tile([P, 512], I32, name="q_i")
-        nc.vector.tensor_copy(out=q_i[:], in_=ang_f)
-        nc.vector.tensor_tensor(out=ang_f, in0=ang_f, in1=q_i[:], op=ALU.subtract)
         ang_abs = const.tile([P, 512], F32, name="ang_abs")
-        nc.vector.scalar_tensor_tensor(out=ang_abs[:], in0=ang_f, scalar=-1.0, in1=ang_f, op0=ALU.mult, op1=ALU.max)
-        quarter = const.tile([P, 1], F32, name="quarter")
-        nc.vector.tensor_scalar(out=quarter[:], in0=one[:], scalar1=math.pi / 2.0, scalar2=None, op0=ALU.mult)
-        eps_t = const.tile([P, 1], F32, name="eps_t")
-        nc.vector.tensor_scalar(out=eps_t[:], in0=one[:], scalar1=EPS, scalar2=None, op0=ALU.mult)
+        halves = (slice(0, 256), slice(256, 512))
+        for h in range(2):
+            rows = slice(8 * h, 8 * h + 8)
+            nc.vector.tensor_tensor(out=ang[:, rows, :], in0=s_f[:, rows].unsqueeze(2).to_broadcast([P, 8, 32]),
+                                    in1=fr[:].unsqueeze(1).to_broadcast([P, 8, 32]), op=ALU.mult)
+        for h in halves:
+            nc.vector.tensor_copy(out=q_i[:, h], in_=ang_f[:, h])
+        for h in halves:
+            nc.vector.tensor_tensor(out=ang_f[:, h], in0=ang_f[:, h], in1=q_i[:, h], op=ALU.subtract)
+        for h in halves:
+            nc.vector.scalar_tensor_tensor(out=ang_abs[:, h], in0=ang_f[:, h], scalar=-1.0, in1=ang_f[:, h], op0=ALU.mult, op1=ALU.max)
         sin_t = const.tile([P, 16, 32], F32, name="sin_t")
         cos_t = const.tile([P, 16, 32], F32, name="cos_t")
         nc.scalar.activation(out=sin_t[:], in_=ang[:], func=ACT.Sin, scale=2.0 * math.pi)
@@ -118,13 +124,15 @@ def tile_modelnew_pb_t_kernel(tc, hidden_states, kv_a_w_ckv, k_pe_raw, kv_a_ln_w
                         nc.tensor.transpose(xt[:, e, v, :], words[:, 256 * g + v:256 * (g + 1):2], ident_f[:])
                 dst = wa_grp[:, g, u * 256:(u + 1) * 256, :].rearrange("p (m e) v -> p m e v", e=2)
                 src = xt[:].rearrange("p e v m -> p m e v")
-                if g == 0:
-                    nc.scalar.copy(out=dst, in_=src)
-                else:
+                if u == 0:
                     nc.vector.tensor_copy(out=dst, in_=src)
-        for g in range(2):
-            nc.vector.quantize_mx(out=wa_c[:, g, :].bitcast(FP8X4), scales=wa_s[:, g, :],
-                                  in_=wa_grp[:, g].rearrange("p n v -> p (n v)").bitcast(BF16))
+                else:
+                    nc.scalar.copy(out=dst, in_=src)
+        for u in range(2):
+            cols = slice(u * 256, (u + 1) * 256)
+            for g in range(2):
+                nc.vector.quantize_mx(out=wa_c[:, g, cols].bitcast(FP8X4), scales=wa_s[:, g, cols],
+                                      in_=wa_grp[:, g, cols].rearrange("p n v -> p (n v)").bitcast(BF16))
 
         w_bc = const.tile([P, 2, P, 2], BF16, name="w_bc")
         wb_grp = const.tile([P, 512, 2], F32, name="wb_grp", align_bytes=64)
@@ -134,6 +142,9 @@ def tile_modelnew_pb_t_kernel(tc, hidden_states, kv_a_w_ckv, k_pe_raw, kv_a_ln_w
         def spread_gain():
             ps = ytp.tile([P, 512], F32, tag="yt")
             nc.tensor.matmul(ps[:], lhsT=ones[:], rhs=w_row[:], start=True, stop=True)
+            return ps
+
+        def keep_gain(ps):
             nc.scalar.copy(out=w_bc[:], in_=ps[:].rearrange("p (m u e) -> p u m e", u=2, e=2))
 
         def prep_wb(a2):
@@ -180,6 +191,13 @@ def tile_modelnew_pb_t_kernel(tc, hidden_states, kv_a_w_ckv, k_pe_raw, kv_a_ln_w
                 nc.gpsimd.tensor_scalar(out=key_sb[c][:, 1, js, 128:192], in0=key_sb[c][:, 0, js, 128:192],
                                         scalar1=1.0, scalar2=0.0, op0=ALU.mult, op1=ALU.add)
 
+        sorted_words = {}
+
+        def sort_words(q, i):
+            dst = work.tile([P, 2, 2, P], F32, tag="sw", name="sw", bufs=4)
+            nc.vector.tensor_copy(out=dst[:], in_=hs_sb[q][:, i, :].bitcast(F32).rearrange("p (g w v) -> p g v w", g=2, v=2))
+            sorted_words[q, i] = dst
+
         def t1(q):
             xtd[q] = []
             for i in range(2):
@@ -187,14 +205,18 @@ def tile_modelnew_pb_t_kernel(tc, hidden_states, kv_a_w_ckv, k_pe_raw, kv_a_ln_w
                 words = hs_sb[q][:, i, :].bitcast(F32)
                 for g in range(2):
                     for v in range(2):
-                        nc.tensor.transpose(xt[:, g, v, :], words[:, 256 * g + v:256 * (g + 1):2], ident_f[:])
+                        if (q, i) in sorted_words:
+                            src = sorted_words[q, i][:, g, v, :]
+                        else:
+                            src = words[:, 256 * g + v:256 * (g + 1):2]
+                        nc.tensor.transpose(xt[:, g, v, :], src, ident_f[:])
                 xtd[q].append(xt)
 
         def pass1(q, i):
             if i == 0:
                 grp[q] = work.tile([P, 2, 2, P, 2], F32, tag="grp", name="grp", align_bytes=64)
             src = xtd[q][i][:].rearrange("p g v r -> p g r v")
-            if q == 0 or (i == 1 and q % 4 == 3):
+            if q == 0 or (i == 1 and q % 2 == 1):
                 nc.scalar.copy(out=grp[q][:, i], in_=src)
             else:
                 nc.vector.tensor_copy(out=grp[q][:, i], in_=src)
@@ -202,8 +224,14 @@ def tile_modelnew_pb_t_kernel(tc, hidden_states, kv_a_w_ckv, k_pe_raw, kv_a_ln_w
         def quant_hs(q):
             hc = work.tile([P, 512], U32, tag="hc", name="hc", align_bytes=64)
             hsc = work.tile([P, 512], U8, tag="hsc", name="hsc", align_bytes=64)
-            nc.vector.quantize_mx(out=hc[:].bitcast(FP8X4), scales=hsc[:],
-                                  in_=grp[q][:].rearrange("p i g r v -> p (i g r v)").bitcast(BF16))
+            if q == 0:
+                for i in range(2):
+                    cols = slice(i * 256, (i + 1) * 256)
+                    nc.vector.quantize_mx(out=hc[:, cols].bitcast(FP8X4), scales=hsc[:, cols],
+                                          in_=grp[q][:, i].rearrange("p g r v -> p (g r v)").bitcast(BF16))
+            else:
+                nc.vector.quantize_mx(out=hc[:].bitcast(FP8X4), scales=hsc[:],
+                                      in_=grp[q][:].rearrange("p i g r v -> p (i g r v)").bitcast(BF16))
             hcode[q] = (hc, hsc)
 
         def s1(q):
@@ -231,8 +259,8 @@ def tile_modelnew_pb_t_kernel(tc, hidden_states, kv_a_w_ckv, k_pe_raw, kv_a_ln_w
         def normalise(q, i):
             if i == 0:
                 ckn[q] = work.tile([P, 2, 512], BF16, tag="ckn", name="ckn")
-            nc.vector.scalar_tensor_tensor(out=ckn[q][:, i, :], in0=ck[q][i][:], scalar=rstd[q][:, i:i + 1],
-                                           in1=w_bc[:].rearrange("p u m e -> p (u m e)"), op0=ALU.mult, op1=ALU.mult)
+            nc.vector.scalar_tensor_tensor(out=ckn[q][:, i, :], in0=w_bc[:].rearrange("p u m e -> p (u m e)"),
+                                           scalar=rstd[q][:, i:i + 1], in1=ck[q][i][:], op0=ALU.mult, op1=ALU.mult)
 
         def t2(q):
             yt = ytp.tile([P, 2, 2, P], F32, tag="yt")
@@ -277,7 +305,7 @@ def tile_modelnew_pb_t_kernel(tc, hidden_states, kv_a_w_ckv, k_pe_raw, kv_a_ln_w
             c, j = divmod(2 * q + i, 4)
             src = kv[q][i][:].rearrange("p (h e d) -> p h e d", h=2, e=2)[:, :, part, :]
             dst = key_sb[c][:, :, j, 0:P] if part == 0 else v_sb[c][:, :, j, :]
-            if q >= N_PAIRS - 3 and i == 0:
+            if q >= N_PAIRS - 3 and i == 0 or q == N_PAIRS - 4:
                 nc.vector.tensor_copy(out=dst, in_=src)
             else:
                 nc.scalar.copy(out=dst, in_=src)
@@ -305,13 +333,13 @@ def tile_modelnew_pb_t_kernel(tc, hidden_states, kv_a_w_ckv, k_pe_raw, kv_a_ln_w
         def live(q):
             return 0 <= q < N_PAIRS
 
-        for r in range(N_PAIRS + 5):
+        for r in range(N_PAIRS + 6):
             if r % 2 == 1 and r // 2 < 8:
                 open_chunk(r // 2)
             if live(r):
                 t1(r)
-            if r == 1:
-                spread_gain()
+            if r == 0:
+                gain = spread_gain()
             if r == 2:
                 prep_wb(0)
                 prep_wb(1)
@@ -319,14 +347,19 @@ def tile_modelnew_pb_t_kernel(tc, hidden_states, kv_a_w_ckv, k_pe_raw, kv_a_ln_w
                 t2(r - 3)
             if live(r):
                 pass1(r, 0)
+            if live(r):
                 pass1(r, 1)
             if r == 0:
                 nc.scalar.activation(out=warm[:], in_=eps_t[:], func=ACT.Abs_reciprocal_sqrt)
+            if r == 0:
+                keep_gain(gain)
             if r - 3 == N_PAIRS - 1:
                 pass4(r - 3, 0)
                 pass4(r - 3, 1)
             elif live(r - 3):
                 pass4(r - 3)
+            if 2 <= r + 1 < N_PAIRS:
+                sort_words(r + 1, 1)
             if r == 3:
                 quant_wb()
             if r - 3 == N_PAIRS - 1:
@@ -347,15 +380,17 @@ def tile_modelnew_pb_t_kernel(tc, hidden_states, kv_a_w_ckv, k_pe_raw, kv_a_ln_w
             if live(r - 1):
                 rsqrt(r - 1, 0)
             if live(r - 4):
-                for part in range(2):
-                    emit(r - 4, 0, part)
-                    store(r - 4, 0, part)
+                emit(r - 4, 0, 0)
+                store(r - 4, 0, 0)
+                emit(r - 4, 0, 1)
+                store(r - 4, 0, 1)
             if live(r - 1):
                 rsqrt(r - 1, 1)
             if live(r - 4):
-                for part in range(2):
-                    emit(r - 4, 1, part)
-                    store(r - 4, 1, part)
+                emit(r - 4, 1, 0)
+                store(r - 4, 1, 0)
+                emit(r - 4, 1, 1)
+                store(r - 4, 1, 1)
             if live(r - 1):
                 normalise(r - 1, 0)
             if live(r - 1):

@@ -171,12 +171,14 @@ def tile_modelnew_pb_t_kernel(tc, hidden_states, kv_a_w_ckv, k_pe_raw, kv_a_ln_w
         g2 = {}
         c2 = {}
         kv = {}
+        both = {}
         key_sb = {}
         v_sb = {}
 
         def open_chunk(c):
-            key_sb[c] = outp.tile([P, 2, 4, 192], F32, tag="key", name="key")
-            v_sb[c] = outp.tile([P, 2, 4, P], F32, tag="v", name="v")
+            both[c] = outp.tile([P, 2, 1728], F32, tag="both", name="both")
+            key_sb[c] = both[c][:, :, 0:768].rearrange("p h (j d) -> p h j d", j=4)
+            v_sb[c] = both[c][:, :, 768:1280].rearrange("p h (j d) -> p h j d", j=4)
             cs = c % 4
             for e in range(2):
                 x = kpe[:, c, e * P:(e + 1) * P].rearrange("p (j h i) -> p j h i", h=2, i=32)
@@ -263,7 +265,10 @@ def tile_modelnew_pb_t_kernel(tc, hidden_states, kv_a_w_ckv, k_pe_raw, kv_a_ln_w
                                            scalar=rstd[q][:, i:i + 1], in1=ck[q][i][:], op0=ALU.mult, op1=ALU.mult)
 
         def t2(q):
-            yt = ytp.tile([P, 2, 2, P], F32, tag="yt")
+            if q == N_PAIRS - 1:
+                yt = accp.tile([P, 2, 2, P], F32, tag="acc")
+            else:
+                yt = ytp.tile([P, 2, 2, P], F32, tag="yt")
             for i in range(2):
                 words = ckn[q][:, i, :].bitcast(F32)
                 for u in range(2):
@@ -295,18 +300,24 @@ def tile_modelnew_pb_t_kernel(tc, hidden_states, kv_a_w_ckv, k_pe_raw, kv_a_ln_w
             cc, csc = c2[q]
             kv[q] = []
             for i in range(2):
-                acc = kvp.tile([P, 512], F32, tag="kv")
+                if q == N_PAIRS - 1:
+                    acc = accp.tile([P, 512], F32, tag="acc")
+                elif q == N_PAIRS - 2:
+                    acc = xtp.tile([P, 512], F32, tag="xt")
+                else:
+                    acc = kvp.tile([P, 512], F32, tag="kv")
                 cols = slice(i * P, (i + 1) * P)
                 nc.tensor.matmul_mx(out=acc[:], lhsT=cc[:, cols].bitcast(FP8X4), lhsT_scale=csc[:, cols],
                                     rhs=wb_c[:].bitcast(FP8X4), rhs_scale=wb_s[:], start=True, stop=True)
                 kv[q].append(acc)
 
-        def emit(q, i, part):
+        def emit(q, i, eng=None):
             c, j = divmod(2 * q + i, 4)
-            src = kv[q][i][:].rearrange("p (h e d) -> p h e d", h=2, e=2)[:, :, part, :]
-            dst = key_sb[c][:, :, j, 0:P] if part == 0 else v_sb[c][:, :, j, :]
-            if q >= N_PAIRS - 3 and i == 0 or q == N_PAIRS - 4:
-                nc.vector.tensor_copy(out=dst, in_=src)
+            src = kv[q][i][:].rearrange("p (h e d) -> p h e d", h=2, e=2)
+            gap = 768 + P * j - 192 * j
+            dst = both[c][:, :, 192 * j:192 * j + 2 * gap].rearrange("p h (e x) -> p h e x", e=2)[:, :, :, 0:P]
+            if eng is not None:
+                eng.tensor_copy(out=dst, in_=src)
             else:
                 nc.scalar.copy(out=dst, in_=src)
 
@@ -316,7 +327,7 @@ def tile_modelnew_pb_t_kernel(tc, hidden_states, kv_a_w_ckv, k_pe_raw, kv_a_ln_w
             rows = slice(cs * 512, (cs + 1) * 512)
             if q == N_PAIRS - 1:
                 js = slice(j, j + 1)
-            elif c >= 6 and i == 1:
+            elif c >= 5 and i == 1:
                 js = slice(j - 1, j + 1)
             elif j == 3:
                 js = slice(0, 4)
@@ -326,14 +337,14 @@ def tile_modelnew_pb_t_kernel(tc, hidden_states, kv_a_w_ckv, k_pe_raw, kv_a_ln_w
             tile = key_sb[c] if part == 0 else v_sb[c]
             view = out[b, :, rows, :].rearrange("h (p j) d -> p h j d", j=4)
             if j == 3 and js.start == 0:
-                nc.sync.dma_start(out=view.rearrange("p h j d -> p h (j d)"), in_=tile[:].rearrange("p h j d -> p h (j d)"))
+                nc.sync.dma_start(out=view.rearrange("p h j d -> p h (j d)"), in_=tile.rearrange("p h j d -> p h (j d)"))
             else:
                 nc.sync.dma_start(out=view[:, :, js, :], in_=tile[:, :, js, :])
 
         def live(q):
             return 0 <= q < N_PAIRS
 
-        for r in range(N_PAIRS + 6):
+        for r in range(N_PAIRS):
             if r % 2 == 1 and r // 2 < 8:
                 open_chunk(r // 2)
             if live(r):
@@ -353,19 +364,13 @@ def tile_modelnew_pb_t_kernel(tc, hidden_states, kv_a_w_ckv, k_pe_raw, kv_a_ln_w
                 nc.scalar.activation(out=warm[:], in_=eps_t[:], func=ACT.Abs_reciprocal_sqrt)
             if r == 0:
                 keep_gain(gain)
-            if r - 3 == N_PAIRS - 1:
-                pass4(r - 3, 0)
-                pass4(r - 3, 1)
-            elif live(r - 3):
+            if live(r - 3):
                 pass4(r - 3)
             if 2 <= r + 1 < N_PAIRS:
                 sort_words(r + 1, 1)
             if r == 3:
                 quant_wb()
-            if r - 3 == N_PAIRS - 1:
-                quant2(r - 3, 0)
-                quant2(r - 3, 1)
-            elif live(r - 3):
+            if live(r - 3):
                 quant2(r - 3)
             if live(r):
                 quant_hs(r)
@@ -380,18 +385,54 @@ def tile_modelnew_pb_t_kernel(tc, hidden_states, kv_a_w_ckv, k_pe_raw, kv_a_ln_w
             if live(r - 1):
                 rsqrt(r - 1, 0)
             if live(r - 4):
-                emit(r - 4, 0, 0)
+                emit(r - 4, 0)
                 store(r - 4, 0, 0)
-                emit(r - 4, 0, 1)
                 store(r - 4, 0, 1)
             if live(r - 1):
                 rsqrt(r - 1, 1)
             if live(r - 4):
-                emit(r - 4, 1, 0)
+                emit(r - 4, 1)
                 store(r - 4, 1, 0)
-                emit(r - 4, 1, 1)
                 store(r - 4, 1, 1)
             if live(r - 1):
                 normalise(r - 1, 0)
             if live(r - 1):
                 normalise(r - 1, 1)
+
+        def out_tile(q, i, eng=None):
+            emit(q, i, eng)
+            store(q, i, 0)
+            store(q, i, 1)
+
+        last = N_PAIRS - 1
+        V = nc.vector
+        t2(last - 2)
+        s1(last)
+        s2(last - 3)
+        pass4(last - 2)
+        quant2(last - 2)
+        t2(last - 1)
+        square(last, 0)
+        square(last, 1)
+        out_tile(last - 3, 0, V)
+        out_tile(last - 3, 1, V)
+        rsqrt(last, 0)
+        pass4(last - 1)
+        rsqrt(last, 1)
+        s2(last - 2)
+        normalise(last, 0)
+        normalise(last, 1)
+        quant2(last - 1)
+        t2(last)
+        out_tile(last - 2, 0)
+        out_tile(last - 2, 1)
+        pass4(last, 0)
+        pass4(last, 1)
+        s2(last - 1)
+        quant2(last, 0)
+        quant2(last, 1)
+        s2(last)
+        out_tile(last - 1, 0)
+        out_tile(last - 1, 1, V)
+        out_tile(last, 0)
+        out_tile(last, 1, V)

@@ -110,8 +110,8 @@ def tile_modelnew_pb_t_kernel(tc, hidden_states, kv_a_w_ckv, k_pe_raw, kv_a_ln_w
         warm = const.tile([P, 1], F32, name="warm")
 
         wa_grp = const.tile([P, 2, 512, 2], F32, name="wa_grp", align_bytes=64)
-        wa_c = const.tile([P, 2, 512], U32, name="wa_c", align_bytes=64)
-        wa_s = const.tile([P, 2, 512], U8, name="wa_s", align_bytes=64)
+        wa_c = const.tile([P, 2, 512], U32, name="wa_c", align_bytes=256)
+        wa_s = const.tile([P, 2, 512], U8, name="wa_s", align_bytes=256)
         for u in range(2):
             for g in range(2):
                 if 2 * u + g < 3:
@@ -136,8 +136,8 @@ def tile_modelnew_pb_t_kernel(tc, hidden_states, kv_a_w_ckv, k_pe_raw, kv_a_ln_w
 
         w_bc = const.tile([P, 2, P, 2], BF16, name="w_bc")
         wb_grp = const.tile([P, 512, 2], F32, name="wb_grp", align_bytes=64)
-        wb_c = const.tile([P, 512], U32, name="wb_c", align_bytes=64)
-        wb_s = const.tile([P, 512], U8, name="wb_s", align_bytes=64)
+        wb_c = const.tile([P, 512], U32, name="wb_c", align_bytes=256)
+        wb_s = const.tile([P, 512], U8, name="wb_s", align_bytes=256)
 
         def spread_gain():
             ps = ytp.tile([P, 512], F32, tag="yt")
@@ -224,8 +224,8 @@ def tile_modelnew_pb_t_kernel(tc, hidden_states, kv_a_w_ckv, k_pe_raw, kv_a_ln_w
                 nc.vector.tensor_copy(out=grp[q][:, i], in_=src)
 
         def quant_hs(q):
-            hc = work.tile([P, 512], U32, tag="hc", name="hc", align_bytes=64)
-            hsc = work.tile([P, 512], U8, tag="hsc", name="hsc", align_bytes=64)
+            hc = work.tile([P, 512], U32, tag="hc", name="hc", align_bytes=256)
+            hsc = work.tile([P, 512], U8, tag="hsc", name="hsc", align_bytes=256)
             if q == 0:
                 for i in range(2):
                     cols = slice(i * 256, (i + 1) * 256)
@@ -287,8 +287,8 @@ def tile_modelnew_pb_t_kernel(tc, hidden_states, kv_a_w_ckv, k_pe_raw, kv_a_ln_w
 
         def quant2(q, i=None):
             if not i:
-                cc = work.tile([P, 256], U32, tag="cc", name="cc", align_bytes=64)
-                csc = work.tile([P, 256], U8, tag="csc", name="csc", align_bytes=64)
+                cc = work.tile([P, 256], U32, tag="cc", name="cc", align_bytes=256)
+                csc = work.tile([P, 256], U8, tag="csc", name="csc", align_bytes=256)
                 c2[q] = (cc, csc)
             cc, csc = c2[q]
             s = slice(0, 2) if i is None else slice(i, i + 1)

from contextlib import ExitStack
import math

import concourse.mybir as mybir
from concourse.masks import make_identity

FLOPS = 2 * 4096 * 1024 * 512 + 2 * 4096 * 512 * 512

F32 = mybir.dt.float32
BF16 = mybir.dt.bfloat16
I32 = mybir.dt.int32
U32 = mybir.dt.uint32
U8 = mybir.dt.uint8
FP8X4 = mybir.dt.float8_e4m3fn_x4
ALU = mybir.AluOpType
ACT = mybir.ActivationFunctionType

P = 128
EPS = 1e-6
THETA = 10000.0
N_PAIRS = 16


def tile_modelnew_pb_t_kernel(tc, hidden_states, kv_a_w_ckv, k_pe_raw, kv_a_ln_w, kv_b_w, out_0, out_1):
    nc = tc.nc
    with ExitStack() as ctx:
        const = ctx.enter_context(tc.tile_pool(name="const", bufs=1))
        work = ctx.enter_context(tc.tile_pool(name="work", bufs=3))
        outp = ctx.enter_context(tc.tile_pool(name="outp", bufs=4))
        xtp = ctx.enter_context(tc.psum_pool(name="xtp", bufs=2))
        accp = ctx.enter_context(tc.psum_pool(name="accp", bufs=3))
        ytp = ctx.enter_context(tc.psum_pool(name="ytp", bufs=1))
        kvp = ctx.enter_context(tc.psum_pool(name="kvp", bufs=2))
        ctx.enter_context(tc.manual_schedule())

        s_i = const.tile([P, 16], I32, name="s_i")
        nc.gpsimd.iota(s_i[:], pattern=[[512, 4], [1, 4]], base=0, channel_multiplier=4)
        ident_f = const.tile([P, P], F32, name="ident_f")
        make_identity(nc, ident_f[:])
        w_row = const.tile([P, 512], BF16, name="w_row")
        nc.gpsimd.memset(w_row[:], 0.0)
        ones = const.tile([P, P], BF16, name="ones")
        nc.gpsimd.memset(ones[:], 1.0)

        one = const.tile([P, 1], F32, name="one")
        nc.vector.memset(one[:], 1.0)
        warm0 = const.tile([P, 1], F32, name="warm0")
        nc.scalar.activation(out=warm0[:], in_=one[:], func=ACT.Sin)

        hs_v = hidden_states.flatten_outer_dims().rearrange("(c p j) d -> c p (j d)", p=P, j=4)
        wa_sb = []
        for a in range(4):
            wa_a = const.tile([P, 1024], BF16, name="wa%d" % a)
            wa_sb.append(wa_a)
        wb_sb = const.tile([P, 4, 512], BF16, name="wb_sb")
        kpe = const.tile([P, 8, 256], BF16, name="kpe")
        hs_sb = []
        for q in range(N_PAIRS):
            hs_q = const.tile([P, 2, 1024], BF16, name="hs%d" % q)
            hs_sb.append(hs_q)

        def load_hs(q):
            c, e = divmod(q, 2)
            nc.sync.dma_start(out=hs_sb[q][:].rearrange("p j d -> p (j d)"), in_=hs_v[c][:, e * 2048:(e + 1) * 2048])

        wa_v = kv_a_w_ckv.rearrange("(p a) d -> a p d", a=4)
        for a in range(4):
            nc.sync.dma_start(out=wa_sb[a][:], in_=wa_v[a])
        for j in range(2):
            nc.sync.dma_start(out=hs_sb[0][:, j, :], in_=hs_v[0][:, j * 1024:(j + 1) * 1024])
        nc.sync.dma_start(out=w_row[0:1, :], in_=kv_a_ln_w.rearrange("(a n) -> a n", a=1))
        load_hs(1)
        nc.sync.dma_start(out=wb_sb[:], in_=kv_b_w.rearrange("(a p) k -> p a k", p=P))
        load_hs(2)
        load_hs(3)
        nc.sync.dma_start(out=kpe[:], in_=k_pe_raw.flatten_outer_dims().rearrange("(c p j) r -> p c (j r)", p=P, j=4))
        for q in range(4, N_PAIRS):
            load_hs(q)

        s_f = const.tile([P, 16], F32, name="s_f")
        nc.vector.tensor_copy(out=s_f[:], in_=s_i[:])
        fr = const.tile([P, 32], F32, name="fr")
        for i in range(4):
            nc.vector.tensor_scalar(out=fr[:, i:i + 1], in0=one[:], scalar1=THETA ** (-i / 32.0) / (2.0 * math.pi), scalar2=None, op0=ALU.mult)
        eps_t = const.tile([P, 1], F32, name="eps_t")
        nc.vector.tensor_scalar(out=eps_t[:], in0=one[:], scalar1=EPS, scalar2=None, op0=ALU.mult)
        quarter = const.tile([P, 1], F32, name="quarter")
        nc.vector.tensor_scalar(out=quarter[:], in0=one[:], scalar1=math.pi / 2.0, scalar2=None, op0=ALU.mult)
        for n in (4, 8, 16):
            nc.vector.tensor_scalar(out=fr[:, n:2 * n], in0=fr[:, 0:n], scalar1=THETA ** (-n / 32.0), scalar2=None, op0=ALU.mult)
        ang = const.tile([P, 16, 32], F32, name="ang")
        ang_f = ang[:].rearrange("p s i -> p (s i)")
        q_i = const.tile([P, 512], I32, name="q_i")
        ang_abs = const.tile([P, 512], F32, name="ang_abs")
        halves = (slice(0, 256), slice(256, 512))
        for h in range(2):
            rows = slice(8 * h, 8 * h + 8)
            nc.vector.tensor_tensor(out=ang[:, rows, :], in0=s_f[:, rows].unsqueeze(2).to_broadcast([P, 8, 32]),
                                    in1=fr[:].unsqueeze(1).to_broadcast([P, 8, 32]), op=ALU.mult)
        for h in halves:
            nc.vector.tensor_copy(out=q_i[:, h], in_=ang_f[:, h])
        for h in halves:
            nc.vector.tensor_tensor(out=ang_f[:, h], in0=ang_f[:, h], in1=q_i[:, h], op=ALU.subtract)
        for h in halves:
            nc.vector.scalar_tensor_tensor(out=ang_abs[:, h], in0=ang_f[:, h], scalar=-1.0, in1=ang_f[:, h], op0=ALU.mult, op1=ALU.max)
        sin_t = const.tile([P, 16, 32], F32, name="sin_t")
        cos_t = const.tile([P, 16, 32], F32, name="cos_t")
        nc.scalar.activation(out=sin_t[:], in_=ang[:], func=ACT.Sin, scale=2.0 * math.pi)
        nc.scalar.activation(out=cos_t[:].rearrange("p s i -> p (s i)"), in_=ang_abs[:], func=ACT.Sin, scale=-2.0 * math.pi, bias=quarter[:, 0:1])
        warm = const.tile([P, 1], F32, name="warm")

        wa_grp = const.tile([P, 2, 512, 2], F32, name="wa_grp", align_bytes=64)
        wa_c = const.tile([P, 2, 512], U32, name="wa_c", align_bytes=256)
        wa_s = const.tile([P, 2, 512], U8, name="wa_s", align_bytes=256)
        for u in range(2):
            for g in range(2):
                if 2 * u + g < 3:
                    xt = accp.tile([P, 2, 2, P], F32, tag="acc")
                else:
                    xt = kvp.tile([P, 2, 2, P], F32, tag="kv")
                for e in range(2):
                    words = wa_sb[2 * u + e][:].bitcast(F32)
                    for v in range(2):
                        nc.tensor.transpose(xt[:, e, v, :], words[:, 256 * g + v:256 * (g + 1):2], ident_f[:])
                dst = wa_grp[:, g, u * 256:(u + 1) * 256, :].rearrange("p (m e) v -> p m e v", e=2)
                src = xt[:].rearrange("p e v m -> p m e v")
                if u == 0:
                    nc.vector.tensor_copy(out=dst, in_=src)
                else:
                    nc.scalar.copy(out=dst, in_=src)
        for u in range(2):
            cols = slice(u * 256, (u + 1) * 256)
            for g in range(2):
                nc.vector.quantize_mx(out=wa_c[:, g, cols].bitcast(FP8X4), scales=wa_s[:, g, cols],
                                      in_=wa_grp[:, g, cols].rearrange("p n v -> p (n v)").bitcast(BF16))

        w_bc = const.tile([P, 2, P, 2], BF16, name="w_bc")
        wb_grp = const.tile([P, 512, 2], F32, name="wb_grp", align_bytes=64)
        wb_c = const.tile([P, 512], U32, name="wb_c", align_bytes=256)
        wb_s = const.tile([P, 512], U8, name="wb_s", align_bytes=256)

        def spread_gain():
            ps = ytp.tile([P, 512], F32, tag="yt")
            nc.tensor.matmul(ps[:], lhsT=ones[:], rhs=w_row[:], start=True, stop=True)
            return ps

        def keep_gain(ps):
            nc.scalar.copy(out=w_bc[:], in_=ps[:].rearrange("p (m u e) -> p u m e", u=2, e=2))

        def prep_wb(a2):
            xt = kvp.tile([P, 2, 2, P], F32, tag="kv")
            for a in range(2):
                words = wb_sb[:, 2 * a2 + a, :].bitcast(F32)
                for v in range(2):
                    nc.tensor.transpose(xt[:, a, v, :], words[:, v:256:2], ident_f[:])
            nc.scalar.copy(out=wb_grp[:, a2 * 256:(a2 + 1) * 256, :].rearrange("p (a r) v -> p a r v", a=2),
                           in_=xt[:].rearrange("p a v r -> p a r v"))

        def quant_wb():
            nc.vector.quantize_mx(out=wb_c[:].bitcast(FP8X4), scales=wb_s[:],
                                  in_=wb_grp[:].rearrange("p n v -> p (n v)").bitcast(BF16))

        xtd = {}
        grp = {}
        hcode = {}
        ck = {}
        rstd = {}
        ssq = {}
        ckn = {}
        ytd = {}
        g2 = {}
        c2 = {}
        kv = {}
        both = {}
        key_sb = {}
        v_sb = {}

        def open_chunk(c):
            both[c] = outp.tile([P, 2, 1728], F32, tag="both", name="both")
            key_sb[c] = both[c][:, :, 0:768].rearrange("p h (j d) -> p h j d", j=4)
            v_sb[c] = both[c][:, :, 768:1280].rearrange("p h (j d) -> p h j d", j=4)
            cs = c % 4
            for e in range(2):
                x = kpe[:, c, e * P:(e + 1) * P].rearrange("p (j h i) -> p j h i", h=2, i=32)
                rows = slice(4 * cs + 2 * e, 4 * cs + 2 * e + 2)
                js = slice(2 * e, 2 * e + 2)
                ra = work.tile([P, 2, 2, 32], F32, tag="ra", name="ra")
                rb = work.tile([P, 2, 2, 32], F32, tag="rb", name="rb")
                nc.gpsimd.tensor_tensor(out=ra[:], in0=x, in1=cos_t[:, rows, :].unsqueeze(2).to_broadcast([P, 2, 2, 32]), op=ALU.mult)
                nc.gpsimd.tensor_tensor(out=rb[:], in0=x, in1=sin_t[:, rows, :].unsqueeze(2).to_broadcast([P, 2, 2, 32]), op=ALU.mult)
                nc.gpsimd.tensor_tensor(out=key_sb[c][:, 0, js, 128:160], in0=ra[:, :, 0, :], in1=rb[:, :, 1, :], op=ALU.subtract)
                nc.gpsimd.tensor_tensor(out=key_sb[c][:, 0, js, 160:192], in0=ra[:, :, 1, :], in1=rb[:, :, 0, :], op=ALU.add)
                nc.gpsimd.tensor_scalar(out=key_sb[c][:, 1, js, 128:192], in0=key_sb[c][:, 0, js, 128:192],
                                        scalar1=1.0, scalar2=0.0, op0=ALU.mult, op1=ALU.add)

        sorted_words = {}

        def sort_words(q, i):
            dst = work.tile([P, 2, 2, P], F32, tag="sw", name="sw", bufs=4)
            nc.vector.tensor_copy(out=dst[:], in_=hs_sb[q][:, i, :].bitcast(F32).rearrange("p (g w v) -> p g v w", g=2, v=2))
            sorted_words[q, i] = dst

        def t1(q):
            xtd[q] = []
            for i in range(2):
                xt = xtp.tile([P, 2, 2, P], F32, tag="xt")
                words = hs_sb[q][:, i, :].bitcast(F32)
                for g in range(2):
                    for v in range(2):
                        if (q, i) in sorted_words:
                            src = sorted_words[q, i][:, g, v, :]
                        else:
                            src = words[:, 256 * g + v:256 * (g + 1):2]
                        nc.tensor.transpose(xt[:, g, v, :], src, ident_f[:])
                xtd[q].append(xt)

        def pass1(q, i):
            if i == 0:
                grp[q] = work.tile([P, 2, 2, P, 2], F32, tag="grp", name="grp", align_bytes=64)
            src = xtd[q][i][:].rearrange("p g v r -> p g r v")
            if q == 0 or (i == 1 and q % 2 == 1):
                nc.scalar.copy(out=grp[q][:, i], in_=src)
            else:
                nc.vector.tensor_copy(out=grp[q][:, i], in_=src)

        def quant_hs(q):
            hc = work.tile([P, 512], U32, tag="hc", name="hc", align_bytes=256)
            hsc = work.tile([P, 512], U8, tag="hsc", name="hsc", align_bytes=256)
            if q == 0:
                for i in range(2):
                    cols = slice(i * 256, (i + 1) * 256)
                    nc.vector.quantize_mx(out=hc[:, cols].bitcast(FP8X4), scales=hsc[:, cols],
                                          in_=grp[q][:, i].rearrange("p g r v -> p (g r v)").bitcast(BF16))
            else:
                nc.vector.quantize_mx(out=hc[:].bitcast(FP8X4), scales=hsc[:],
                                      in_=grp[q][:].rearrange("p i g r v -> p (i g r v)").bitcast(BF16))
            hcode[q] = (hc, hsc)

        def s1(q):
            hc, hsc = hcode[q]
            ck[q] = []
            for i in range(2):
                acc = accp.tile([P, 512], F32, tag="acc")
                for g in range(2):
                    cols = slice((2 * i + g) * P, (2 * i + g + 1) * P)
                    nc.tensor.matmul_mx(out=acc[:], lhsT=hc[:, cols].bitcast(FP8X4), lhsT_scale=hsc[:, cols],
                                        rhs=wa_c[:, g, :].bitcast(FP8X4), rhs_scale=wa_s[:, g, :], start=(g == 0), stop=(g == 1))
                ck[q].append(acc)

        def square(q, i):
            if i == 0:
                ssq[q] = work.tile([P, 2], F32, tag="ssq", name="ssq")
                rstd[q] = work.tile([P, 2], F32, tag="rs", name="rs")
            junk = work.tile([P, 512], BF16, tag="junk", name="junk")
            nc.scalar.activation(out=junk[:], in_=ck[q][i][:], func=ACT.Square, accum_out=ssq[q][:, i:i + 1])

        def rsqrt(q, i):
            nc.scalar.activation(out=rstd[q][:, i:i + 1], in_=ssq[q][:, i:i + 1], func=ACT.Abs_reciprocal_sqrt,
                                 scale=1.0 / 512.0, bias=eps_t[:, 0:1])

        def normalise(q, i):
            if i == 0:
                ckn[q] = work.tile([P, 2, 512], BF16, tag="ckn", name="ckn")
            nc.vector.scalar_tensor_tensor(out=ckn[q][:, i, :], in0=w_bc[:].rearrange("p u m e -> p (u m e)"),
                                           scalar=rstd[q][:, i:i + 1], in1=ck[q][i][:], op0=ALU.mult, op1=ALU.mult)

        def t2(q):
            if q == N_PAIRS - 1:
                yt = accp.tile([P, 2, 2, P], F32, tag="acc")
            else:
                yt = ytp.tile([P, 2, 2, P], F32, tag="yt")
            for i in range(2):
                words = ckn[q][:, i, :].bitcast(F32)
                for u in range(2):
                    nc.tensor.transpose(yt[:, i, u, :], words[:, u * P:(u + 1) * P], ident_f[:])
            ytd[q] = yt

        def pass4(q, i=None):
            if not i:
                g2[q] = work.tile([P, 2, P, 2], F32, tag="g2", name="g2", align_bytes=64)
            s = slice(0, 2) if i is None else slice(i, i + 1)
            src = ytd[q][:, s].rearrange("p i u r -> p i r u")
            if i == 0:
                nc.vector.tensor_copy(out=g2[q][:, s], in_=src)
            else:
                nc.scalar.copy(out=g2[q][:, s], in_=src)

        def quant2(q, i=None):
            if not i:
                cc = work.tile([P, 256], U32, tag="cc", name="cc", align_bytes=256)
                csc = work.tile([P, 256], U8, tag="csc", name="csc", align_bytes=256)
                c2[q] = (cc, csc)
            cc, csc = c2[q]
            s = slice(0, 2) if i is None else slice(i, i + 1)
            cols = slice(0, 256) if i is None else slice(i * P, (i + 1) * P)
            nc.vector.quantize_mx(out=cc[:, cols].bitcast(FP8X4), scales=csc[:, cols],
                                  in_=g2[q][:, s].rearrange("p i r u -> p (i r u)").bitcast(BF16))

        def s2(q):
            cc, csc = c2[q]
            kv[q] = []
            for i in range(2):
                if q == N_PAIRS - 1:
                    acc = accp.tile([P, 512], F32, tag="acc")
                elif q == N_PAIRS - 2:
                    acc = xtp.tile([P, 512], F32, tag="xt")
                else:
                    acc = kvp.tile([P, 512], F32, tag="kv")
                cols = slice(i * P, (i + 1) * P)
                nc.tensor.matmul_mx(out=acc[:], lhsT=cc[:, cols].bitcast(FP8X4), lhsT_scale=csc[:, cols],
                                    rhs=wb_c[:].bitcast(FP8X4), rhs_scale=wb_s[:], start=True, stop=True)
                kv[q].append(acc)

        def emit(q, i, eng=None):
            c, j = divmod(2 * q + i, 4)
            src = kv[q][i][:].rearrange("p (h e d) -> p h e d", h=2, e=2)
            gap = 768 + P * j - 192 * j
            dst = both[c][:, :, 192 * j:192 * j + 2 * gap].rearrange("p h (e x) -> p h e x", e=2)[:, :, :, 0:P]
            if eng is not None:
                eng.tensor_copy(out=dst, in_=src)
            else:
                nc.scalar.copy(out=dst, in_=src)

        def store(q, i, part):
            c, j = divmod(2 * q + i, 4)
            b, cs = divmod(c, 4)
            rows = slice(cs * 512, (cs + 1) * 512)
            if q == N_PAIRS - 1:
                js = slice(j, j + 1)
            elif c >= 5 and i == 1:
                js = slice(j - 1, j + 1)
            elif j == 3:
                js = slice(0, 4)
            else:
                return
            out = out_0 if part == 0 else out_1
            tile = key_sb[c] if part == 0 else v_sb[c]
            view = out[b, :, rows, :].rearrange("h (p j) d -> p h j d", j=4)
            if j == 3 and js.start == 0:
                nc.sync.dma_start(out=view.rearrange("p h j d -> p h (j d)"), in_=tile.rearrange("p h j d -> p h (j d)"))
            else:
                nc.sync.dma_start(out=view[:, :, js, :], in_=tile[:, :, js, :])

        def live(q):
            return 0 <= q < N_PAIRS

        for r in range(N_PAIRS):
            if r % 2 == 1 and r // 2 < 8:
                open_chunk(r // 2)
            if live(r):
                t1(r)
            if r == 0:
                gain = spread_gain()
            if r == 2:
                prep_wb(0)
                prep_wb(1)
            if live(r - 3):
                t2(r - 3)
            if live(r):
                pass1(r, 0)
            if live(r):
                pass1(r, 1)
            if r == 0:
                nc.scalar.activation(out=warm[:], in_=eps_t[:], func=ACT.Abs_reciprocal_sqrt)
            if r == 0:
                keep_gain(gain)
            if live(r - 3):
                pass4(r - 3)
            if 2 <= r + 1 < N_PAIRS:
                sort_words(r + 1, 1)
            if r == 3:
                quant_wb()
            if live(r - 3):
                quant2(r - 3)
            if live(r):
                quant_hs(r)
            if live(r - 1):
                s1(r - 1)
            if live(r - 4):
                s2(r - 4)
            if live(r - 1):
                square(r - 1, 0)
            if live(r - 1):
                square(r - 1, 1)
            if live(r - 1):
                rsqrt(r - 1, 0)
            if live(r - 4):
                emit(r - 4, 0)
                store(r - 4, 0, 0)
                store(r - 4, 0, 1)
            if live(r - 1):
                rsqrt(r - 1, 1)
            if live(r - 4):
                emit(r - 4, 1)
                store(r - 4, 1, 0)
                store(r - 4, 1, 1)
            if live(r - 1):
                normalise(r - 1, 0)
            if live(r - 1):
                normalise(r - 1, 1)

        def out_tile(q, i, eng=None):
            emit(q, i, eng)
            store(q, i, 0)
            store(q, i, 1)

        last = N_PAIRS - 1
        V = nc.vector
        t2(last - 2)
        s1(last)
        s2(last - 3)
        pass4(last - 2)
        quant2(last - 2)
        t2(last - 1)
        square(last, 0)
        square(last, 1)
        out_tile(last - 3, 0, V)
        out_tile(last - 3, 1, V)
        rsqrt(last, 0)
        pass4(last - 1)
        rsqrt(last, 1)
        s2(last - 2)
        normalise(last, 0)
        normalise(last, 1)
        quant2(last - 1)
        t2(last)
        out_tile(last - 2, 0)
        out_tile(last - 2, 1)
        pass4(last, 0)
        pass4(last, 1)
        s2(last - 1)
        quant2(last, 0)
        quant2(last, 1)
        s2(last)
        out_tile(last - 1, 0)
        out_tile(last - 1, 1, V)
        out_tile(last, 0)
        out_tile(last, 1, V)
